import numpy as np
import ml_dtypes


def mxq(x, axis, fmt="e4m3"):
    dtype, down = {"e4m3": (ml_dtypes.float8_e4m3fn, 7), "e5m2": (ml_dtypes.float8_e5m2, 14)}[fmt]
    v = np.moveaxis(np.asarray(x, np.float32).astype(ml_dtypes.bfloat16).astype(np.float64), axis, -1)
    blocks = v.reshape(v.shape[:-1] + (-1, 32))
    amax = np.abs(blocks).max(-1, keepdims=True)
    byte = np.maximum(np.where(amax > 0, np.frexp(amax)[1] - 1 + 127, 0) - down, 1)
    scale = np.exp2(byte - 127.0)
    codes = (blocks / scale).astype(np.float32).astype(dtype).astype(np.float64)
    return np.moveaxis((codes * scale).reshape(v.shape), -1, axis)


WIDE = False


def mx_kscale(k):
    if not WIDE:
        return np.ones(k)
    levels = np.array([10, -10, 5, -5, 0])
    a = np.random.permutation(np.resize(levels, k // 512 * 4)).reshape(k // 512, 4)
    idx = np.arange(k)
    return np.exp2(a[idx // 512, idx % 128 // 32])


BF16 = ml_dtypes.bfloat16


def bf(x):
    return np.asarray(x, np.float32).astype(BF16)


def f64(x):
    return np.asarray(x).astype(np.float64)


B, C, T, H, W, AT, AF = 1, 512, 16, 14, 14, 64, 128
D = C // 2
C2 = 2 * C
NKV = AT * AF
REP, REM = AT // T, AT % T
QS = np.sqrt(2.0 / np.sqrt(D))


def setup_inputs():
    s = mx_kscale(C2)
    sa, sv = s[:C], s[C:]
    m = np.random.standard_normal((B, C, T))[..., None, None]
    return {"v": bf((np.random.standard_normal((B, C, T, H, W)) + 0.7 * m) * sv[None, :, None, None, None]),
            "a": bf(np.random.standard_normal((B, C, AT, AF)) * sa[None, :, None, None]),
            "Wp": bf(np.random.standard_normal((D, C2)) * 0.8 * QS / np.sqrt(C) / s[None, :]),
            "bp": bf(np.random.standard_normal(D) * 0.1),
            "Wg": bf(np.random.standard_normal((D, C2)) / np.sqrt(C) / s[None, :]),
            "bg": bf(np.random.standard_normal(D) * 0.1)}


def reference(v, a, Wp, bp, Wg, bg):
    z = f64(v).mean(axis=(3, 4))
    z = np.repeat(z, REP, axis=2)
    if REM:
        z = np.concatenate([z, np.broadcast_to(z[:, :, -1:], (B, C, REM))], axis=2)
    z = np.broadcast_to(z[..., None], (B, C, AT, AF))
    av = np.concatenate([f64(a), z], axis=1).reshape(B, C2, NKV)
    avq = mxq(av, 1, "e4m3")
    phi_av = (mxq(f64(Wp), 1, "e4m3") @ avq) + f64(bp)[:, None]
    g_av = (mxq(f64(Wg), 1, "e4m3") @ avq) + f64(bg)[:, None]
    return phi_av, g_av.transpose(0, 2, 1)

@@ -1,0 +1,310 @@
+import concourse.mybir as mybir
+from concourse.masks import make_identity
+
+BF16 = mybir.dt.bfloat16
+F32 = mybir.dt.float32
+U32 = mybir.dt.uint32
+U8 = mybir.dt.uint8
+FP8X4 = mybir.dt.float8_e4m3fn_x4
+ADD = mybir.AluOpType.add
+MULT = mybir.AluOpType.mult
+IDENTITY = mybir.ActivationFunctionType.Identity
+AXIS_X = mybir.AxisListType.X
+
+P = 128
+PACK = 4
+K_PASS = P * PACK
+PASSES = 2
+T = 16
+H = 14
+W = 14
+N = 8192
+STEP = N // T
+D = 256
+D_TILES = D // P
+ROWS = STEP // P
+Z_COPIES = 4
+ZZ_STEPS = 4
+FIRST_PIECE = 2
+VECTOR_COLS = 64
+
+FLOPS = 2 * 2 * D * PASSES * K_PASS * N
+
+
+def tile_nlgate_pa_t_kernel(tc, v, a, Wp, bp, Wg, bg, out_0, out_1):
+    nc = tc.nc
+
+    a_rows = a[0].rearrange("(p j) i f -> p j (i f)", j=PACK)
+    v_rows = v[0].rearrange("(p j) t h w -> p j (t h w)", j=PACK)
+    phi_out = out_0[0].rearrange("(m p) n -> p m n", p=P)
+    g_out = out_1[0].rearrange("(t c r) d -> t c (r d)", c=P, r=ROWS)
+
+    with tc.tile_pool(name="resident", bufs=1) as resident, tc.tile_pool(
+        name="grouped_pool", bufs=4
+    ) as grouped_pool, tc.tile_pool(name="phi_pool", bufs=3) as phi_pool, tc.tile_pool(
+        name="g_pool", bufs=6
+    ) as g_pool:
+        w_raw = {}
+        for name, w in (("p", Wp), ("g", Wg)):
+            raw = resident.tile([P, D_TILES, PASSES * K_PASS], BF16, name="w_raw_%s" % name)
+            nc.sync.dma_start(out=raw[:], in_=w.rearrange("(m p) k -> p m k", p=P))
+            w_raw[name] = raw
+
+        v_raw = []
+        for half in range(2):
+            raw = resident.tile([P, 2, T * H * W], BF16, name="v_raw_%d" % half)
+            nc.sync.dma_start(out=raw[:], in_=v_rows[:, 2 * half : 2 * half + 2, :])
+            v_raw.append(raw)
+
+        bias_rows = resident.tile([P, 2 * D], BF16)
+        nc.vector.memset(bias_rows[:], 0.0)
+        nc.sync.dma_start(out=bias_rows[0:1, 0:D], in_=bp.unsqueeze(0))
+        nc.sync.dma_start(out=bias_rows[0:1, D : 2 * D], in_=bg.unsqueeze(0))
+
+        a_step = []
+        piece_steps = FIRST_PIECE
+        while len(a_step) < T:
+            first = len(a_step)
+            raw = resident.tile([P, PACK, piece_steps * STEP], BF16, name="a_raw_%d" % first)
+            nc.sync.dma_start(
+                out=raw[:], in_=a_rows[:, :, first * STEP : (first + piece_steps) * STEP]
+            )
+            for s in range(piece_steps):
+                a_step.append(raw[:, :, s * STEP : (s + 1) * STEP])
+            piece_steps = len(a_step)
+
+        ones = resident.tile([P, P], BF16)
+        nc.vector.memset(ones[:], 1.0)
+        ident_bf16 = resident.tile([P, P], BF16)
+        make_identity(nc, ident_bf16[:])
+        ident_f32 = resident.tile([P, P], F32)
+        make_identity(nc, ident_f32[:])
+
+        w_codes = {}
+        w_scales = {}
+        for name in ("p", "g"):
+            w_codes[name] = resident.tile(
+                [P, PASSES * D], U32, name="w_codes_%s" % name, align_bytes=64
+            )
+            w_scales[name] = resident.tile(
+                [P, PASSES * D], U8, name="w_scales_%s" % name, align_bytes=64
+            )
+        a_codes = resident.tile([P, N], U32, align_bytes=64)
+        a_scales = resident.tile([P, N], U8, align_bytes=64)
+        zz_codes = resident.tile([P, T * P], U32, align_bytes=64)
+        zz_scales = resident.tile([P, T * P], U8, align_bytes=64)
+        z_codes = resident.tile([P, Z_COPIES * T], U32, align_bytes=64)
+        z_scales = resident.tile([P, Z_COPIES * T], U8, align_bytes=64)
+
+        bg_all = resident.tile([P, D], F32)
+        bp_col = resident.tile([P, D_TILES], F32)
+        phi_bias = resident.tile([P, D_TILES, T], F32)
+        z_sum = resident.tile([P, PACK, T], F32)
+        z_bf16 = resident.tile([P, T, PACK], BF16)
+
+        with tc.psum_pool(name="setup_psum", bufs=1) as setup_psum:
+            for name in ("p", "g"):
+                words = w_raw[name][:].bitcast(F32).rearrange(
+                    "p m (g q u) -> p m g u q", g=PASSES, u=2
+                )
+                w_grouped = grouped_pool.tile(
+                    [P, PASSES, D_TILES, P, PACK], BF16, tag="grouped", align_bytes=64
+                )
+                for g in range(PASSES):
+                    w_t = setup_psum.tile([P, D_TILES, 2, P], F32, tag="w_t", bufs=4)
+                    for m in range(D_TILES):
+                        for u in range(2):
+                            nc.tensor.transpose(w_t[:, m, u, :], words[:, m, g, u, :], ident_f32[:])
+                    grouped_words = w_grouped[:, g].bitcast(F32)
+                    if g == 0:
+                        nc.vector.tensor_copy(
+                            out=grouped_words, in_=w_t[:].rearrange("p m u d -> p m d u")
+                        )
+                    else:
+                        nc.scalar.copy(out=grouped_words, in_=w_t[:].rearrange("p m u d -> p m d u"))
+                nc.vector.quantize_mx(
+                    out=w_codes[name][:].bitcast(FP8X4),
+                    scales=w_scales[name][:],
+                    in_=w_grouped[:].rearrange("p g m d j -> p (g m d j)"),
+                )
+
+            for half in range(2):
+                frames = v_raw[half][:].rearrange("p j (t h w) -> p j t h w", h=H, w=W)
+                row_sum = setup_psum.tile([P, 2, T, W], F32, tag="row_sum", bufs=2)
+                for h in range(H):
+                    nc.tensor.matmul(
+                        out=row_sum[:],
+                        lhsT=ident_bf16[:],
+                        rhs=frames[:, :, :, h, :],
+                        start=(h == 0),
+                        stop=(h == H - 1),
+                    )
+                nc.vector.tensor_reduce(
+                    out=z_sum[:, 2 * half : 2 * half + 2, :], in_=row_sum[:], axis=AXIS_X, op=ADD
+                )
+            nc.vector.tensor_scalar(
+                out=z_bf16[:],
+                in0=z_sum[:].rearrange("p j t -> p t j"),
+                scalar1=1.0 / (H * W),
+                scalar2=None,
+                op0=MULT,
+            )
+
+            bias_psum = setup_psum.tile([P, 2 * D], F32)
+            nc.tensor.matmul(
+                out=bias_psum[:, 0:D], lhsT=ones[:], rhs=bias_rows[:, D : 2 * D], start=True, stop=True
+            )
+            for m in range(D_TILES):
+                nc.tensor.matmul(
+                    out=bias_psum[:, D + 32 * m : D + 32 * (m + 1)],
+                    lhsT=bias_rows[:, m * P : (m + 1) * P],
+                    rhs=ones[:, 0:32],
+                    start=True,
+                    stop=True,
+                )
+            nc.vector.tensor_copy(out=bg_all[:], in_=bias_psum[:, 0:D])
+            nc.vector.tensor_copy(
+                out=bp_col[:],
+                in_=bias_psum[:, D : D + 32 * D_TILES].rearrange("p (m n) -> p m n", n=32)[:, :, 0],
+            )
+
+            z_cols = resident.tile([P, Z_COPIES, T, PACK], BF16, align_bytes=64)
+            nc.vector.tensor_copy(
+                out=z_cols[:], in_=z_bf16[:].unsqueeze(1).to_broadcast([P, Z_COPIES, T, PACK])
+            )
+            nc.vector.quantize_mx(
+                out=z_codes[:].bitcast(FP8X4),
+                scales=z_scales[:],
+                in_=z_cols[:].rearrange("p c t j -> p (c t j)"),
+            )
+            z_phi = setup_psum.tile([P, D_TILES, Z_COPIES * T], F32)
+            for m in range(D_TILES):
+                d_cols = slice(D + m * P, D + (m + 1) * P)
+                nc.tensor.matmul_mx(
+                    out=z_phi[:, m, :],
+                    lhsT=w_codes["p"][:, d_cols].bitcast(FP8X4),
+                    lhsT_scale=w_scales["p"][:, d_cols],
+                    rhs=z_codes[:].bitcast(FP8X4),
+                    rhs_scale=z_scales[:],
+                    start=True,
+                    stop=True,
+                )
+                nc.vector.tensor_scalar(
+                    out=phi_bias[:, m, :],
+                    in0=z_phi[:, m, 0:T],
+                    scalar1=bp_col[:, m : m + 1],
+                    scalar2=None,
+                    op0=ADD,
+                )
+
+            for q in range(T // ZZ_STEPS):
+                zz = grouped_pool.tile([P, ZZ_STEPS, P, PACK], BF16, tag="grouped", align_bytes=64)
+                nc.vector.tensor_copy(
+                    out=zz[:],
+                    in_=z_bf16[:, q * ZZ_STEPS : (q + 1) * ZZ_STEPS, :]
+                    .unsqueeze(2)
+                    .to_broadcast([P, ZZ_STEPS, P, PACK]),
+                )
+                zz_cols = slice(q * ZZ_STEPS * P, (q + 1) * ZZ_STEPS * P)
+                nc.vector.quantize_mx(
+                    out=zz_codes[:, zz_cols].bitcast(FP8X4),
+                    scales=zz_scales[:, zz_cols],
+                    in_=zz[:].rearrange("p t c j -> p (t c j)"),
+                )
+
+        with tc.psum_pool(name="psum", bufs=4, reuse_waits="tile") as psum:
+            grouped_of = {}
+            phi_psum_of = {}
+            g_psum_of = {}
+            phi_stage_of = {}
+
+            def regroup(t):
+                grouped = grouped_pool.tile([P, ROWS, P, PACK], BF16, tag="grouped", align_bytes=64)
+                dst = grouped[:].rearrange("p r m j -> p m j r")
+                src = a_step[t].rearrange("p j (m r) -> p m j r", r=ROWS)
+                nc.vector.tensor_copy(out=dst[:, 0:VECTOR_COLS], in_=src[:, 0:VECTOR_COLS])
+                nc.scalar.copy(out=dst[:, VECTOR_COLS:P], in_=src[:, VECTOR_COLS:P])
+                grouped_of[t] = grouped
+
+            def quantise_and_multiply(t):
+                cols = slice(t * STEP, (t + 1) * STEP)
+                nc.vector.quantize_mx(
+                    out=a_codes[:, cols].bitcast(FP8X4),
+                    scales=a_scales[:, cols],
+                    in_=grouped_of[t][:].rearrange("p r m j -> p (r m j)"),
+                )
+                phi_psum_of[t] = []
+                for m in range(D_TILES):
+                    phi_psum = psum.tile([P, STEP], F32)
+                    d_cols = slice(m * P, (m + 1) * P)
+                    nc.tensor.matmul_mx(
+                        out=phi_psum[:],
+                        lhsT=w_codes["p"][:, d_cols].bitcast(FP8X4),
+                        lhsT_scale=w_scales["p"][:, d_cols],
+                        rhs=a_codes[:, cols].bitcast(FP8X4),
+                        rhs_scale=a_scales[:, cols],
+                        start=True,
+                        stop=True,
+                    )
+                    phi_psum_of[t].append(phi_psum)
+                g_psum_of[t] = []
+                for pair in range(ROWS // 2):
+                    g_psum = psum.tile([P, 2, D], F32)
+                    for i in range(2):
+                        r = 2 * pair + i
+                        n_cols = slice(t * STEP + r * P, t * STEP + (r + 1) * P)
+                        z_cols_t = slice(t * P, (t + 1) * P)
+                        nc.tensor.matmul_mx(
+                            out=g_psum[:, i, :],
+                            lhsT=a_codes[:, n_cols].bitcast(FP8X4),
+                            lhsT_scale=a_scales[:, n_cols],
+                            rhs=w_codes["g"][:, 0:D].bitcast(FP8X4),
+                            rhs_scale=w_scales["g"][:, 0:D],
+                            start=True,
+                            stop=False,
+                        )
+                        nc.tensor.matmul_mx(
+                            out=g_psum[:, i, :],
+                            lhsT=zz_codes[:, z_cols_t].bitcast(FP8X4),
+                            lhsT_scale=zz_scales[:, z_cols_t],
+                            rhs=w_codes["g"][:, D : 2 * D].bitcast(FP8X4),
+                            rhs_scale=w_scales["g"][:, D : 2 * D],
+                            start=False,
+                            stop=True,
+                        )
+                    g_psum_of[t].append(g_psum)
+
+            def finish(t):
+                if t % 2 == 0:
+                    phi_stage = phi_pool.tile([P, D_TILES, 2 * STEP], F32)
+                    phi_stage_of[t // 2] = phi_stage
+                phi_stage = phi_stage_of[t // 2]
+                stage_cols = slice((t % 2) * STEP, (t % 2 + 1) * STEP)
+                for m in range(D_TILES):
+                    nc.scalar.activation(
+                        out=phi_stage[:, m, stage_cols].rearrange("p (c r) -> p c r", r=ROWS),
+                        in_=phi_psum_of[t][m][:].rearrange("p (r c) -> p c r", r=ROWS),
+                        func=IDENTITY,
+                        bias=phi_bias[:, m, t : t + 1],
+                    )
+                if t % 2 == 1:
+                    nc.sync.dma_start(
+                        out=phi_out[:, :, (t - 1) * STEP : (t + 1) * STEP], in_=phi_stage[:]
+                    )
+                g_stage = g_pool.tile([P, ROWS, D], F32)
+                for pair in range(ROWS // 2):
+                    nc.vector.tensor_tensor(
+                        out=g_stage[:, 2 * pair : 2 * pair + 2, :],
+                        in0=g_psum_of[t][pair][:],
+                        in1=bg_all[:].unsqueeze(1).to_broadcast([P, 2, D]),
+                        op=ADD,
+                    )
+                nc.sync.dma_start(out=g_out[t], in_=g_stage[:].rearrange("p r d -> p (r d)"))
+
+            for t in range(-2, T):
+                if t + 2 < T:
+                    regroup(t + 2)
+                if 0 <= t + 1 < T:
+                    quantise_and_multiply(t + 1)
+                if t >= 0:
+                    finish(t)

@@ -5,6 +5,7 @@ BF16 = mybir.dt.bfloat16
 F32 = mybir.dt.float32
 U32 = mybir.dt.uint32
 U8 = mybir.dt.uint8
+I32 = mybir.dt.int32
 FP8X4 = mybir.dt.float8_e4m3fn_x4
 ADD = mybir.AluOpType.add
 MULT = mybir.AluOpType.mult
@@ -24,9 +25,9 @@ D = 256
 D_TILES = D // P
 ROWS = STEP // P
 Z_COPIES = 4
-ZZ_STEPS = 4
 FIRST_PIECE = 2
-VECTOR_COLS = 64
+EARLY_STEPS = 4
+VECTOR_COLS = 48
 
 FLOPS = 2 * 2 * D * PASSES * K_PASS * N
 
@@ -50,20 +51,21 @@ def tile_nlgate_pa_t_kernel(tc, v, a, Wp, bp, Wg, bg, out_0, out_1):
             nc.sync.dma_start(out=raw[:], in_=w.rearrange("(m p) k -> p m k", p=P))
             w_raw[name] = raw
 
-        v_raw = []
-        for half in range(2):
-            raw = resident.tile([P, 2, T * H * W], BF16, name="v_raw_%d" % half)
-            nc.sync.dma_start(out=raw[:], in_=v_rows[:, 2 * half : 2 * half + 2, :])
-            v_raw.append(raw)
+        def load_v_and_biases():
+            for j in range(PACK):
+                nc.sync.dma_start(out=v_raw[:, j, :], in_=v_rows[:, j, :])
+            nc.sync.dma_start(out=bias_rows[0:1, 0:D], in_=bp.unsqueeze(0))
+            nc.sync.dma_start(out=bias_rows[0:1, D : 2 * D], in_=bg.unsqueeze(0))
 
+        v_raw = resident.tile([P, PACK, T * H * W], BF16)
         bias_rows = resident.tile([P, 2 * D], BF16)
         nc.vector.memset(bias_rows[:], 0.0)
-        nc.sync.dma_start(out=bias_rows[0:1, 0:D], in_=bp.unsqueeze(0))
-        nc.sync.dma_start(out=bias_rows[0:1, D : 2 * D], in_=bg.unsqueeze(0))
 
         a_step = []
         piece_steps = FIRST_PIECE
         while len(a_step) < T:
+            if len(a_step) == EARLY_STEPS:
+                load_v_and_biases()
             first = len(a_step)
             raw = resident.tile([P, PACK, piece_steps * STEP], BF16, name="a_raw_%d" % first)
             nc.sync.dma_start(
@@ -100,7 +102,6 @@ def tile_nlgate_pa_t_kernel(tc, v, a, Wp, bp, Wg, bg, out_0, out_1):
         bp_col = resident.tile([P, D_TILES], F32)
         phi_bias = resident.tile([P, D_TILES, T], F32)
         z_sum = resident.tile([P, PACK, T], F32)
-        z_bf16 = resident.tile([P, T, PACK], BF16)
 
         with tc.psum_pool(name="setup_psum", bufs=1) as setup_psum:
             for name in ("p", "g"):
@@ -128,26 +129,34 @@ def tile_nlgate_pa_t_kernel(tc, v, a, Wp, bp, Wg, bg, out_0, out_1):
                     in_=w_grouped[:].rearrange("p g m d j -> p (g m d j)"),
                 )
 
+            frames = v_raw[:].rearrange("p j (t h w) -> p j t h w", h=H, w=W)
             for half in range(2):
-                frames = v_raw[half][:].rearrange("p j (t h w) -> p j t h w", h=H, w=W)
                 row_sum = setup_psum.tile([P, 2, T, W], F32, tag="row_sum", bufs=2)
-                for h in range(H):
-                    nc.tensor.matmul(
-                        out=row_sum[:],
-                        lhsT=ident_bf16[:],
-                        rhs=frames[:, :, :, h, :],
-                        start=(h == 0),
-                        stop=(h == H - 1),
-                    )
+                for i in range(2):
+                    for h in range(H):
+                        nc.tensor.matmul(
+                            out=row_sum[:, i],
+                            lhsT=ident_bf16[:],
+                            rhs=frames[:, 2 * half + i, :, h, :],
+                            start=(h == 0),
+                            stop=(h == H - 1),
+                        )
                 nc.vector.tensor_reduce(
                     out=z_sum[:, 2 * half : 2 * half + 2, :], in_=row_sum[:], axis=AXIS_X, op=ADD
                 )
+            z_cols = resident.tile([P, T, Z_COPIES, PACK], BF16, align_bytes=64)
             nc.vector.tensor_scalar(
-                out=z_bf16[:],
-                in0=z_sum[:].rearrange("p j t -> p t j"),
+                out=z_cols[:],
+                in0=z_sum[:].rearrange("p j t -> p t j").unsqueeze(2).to_broadcast([P, T, Z_COPIES, PACK]),
                 scalar1=1.0 / (H * W),
                 scalar2=None,
                 op0=MULT,
+            )
+            nc.vector.memset(z_scales[:].bitcast(I32), 0)
+            nc.vector.quantize_mx(
+                out=z_codes[:].bitcast(FP8X4),
+                scales=z_scales[:],
+                in_=z_cols[:].rearrange("p t c j -> p (t c j)"),
             )
 
             bias_psum = setup_psum.tile([P, 2 * D], F32)
@@ -168,20 +177,24 @@ def tile_nlgate_pa_t_kernel(tc, v, a, Wp, bp, Wg, bg, out_0, out_1):
                 in_=bias_psum[:, D : D + 32 * D_TILES].rearrange("p (m n) -> p m n", n=32)[:, :, 0],
             )
 
-            z_cols = resident.tile([P, Z_COPIES, T, PACK], BF16, align_bytes=64)
             nc.vector.tensor_copy(
-                out=z_cols[:], in_=z_bf16[:].unsqueeze(1).to_broadcast([P, Z_COPIES, T, PACK])
+                out=zz_codes[:].bitcast(I32).rearrange("p (t b c) -> p t b c", t=T, c=Z_COPIES),
+                in_=z_codes[:]
+                .bitcast(I32)
+                .rearrange("p (t c) -> p t c", c=Z_COPIES)
+                .unsqueeze(2)
+                .to_broadcast([P, T, P // Z_COPIES, Z_COPIES]),
             )
-            nc.vector.quantize_mx(
-                out=z_codes[:].bitcast(FP8X4),
-                scales=z_scales[:],
-                in_=z_cols[:].rearrange("p c t j -> p (c t j)"),
+            nc.vector.tensor_copy(
+                out=zz_scales[:].bitcast(I32).rearrange("p (t b) -> p t b", t=T),
+                in_=z_scales[:].bitcast(I32).unsqueeze(2).to_broadcast([P, T, P // Z_COPIES]),
             )
-            z_phi = setup_psum.tile([P, D_TILES, Z_COPIES * T], F32)
+
+            z_phi = setup_psum.tile([P, D_TILES, T, Z_COPIES], F32)
             for m in range(D_TILES):
                 d_cols = slice(D + m * P, D + (m + 1) * P)
                 nc.tensor.matmul_mx(
-                    out=z_phi[:, m, :],
+                    out=z_phi[:, m],
                     lhsT=w_codes["p"][:, d_cols].bitcast(FP8X4),
                     lhsT_scale=w_scales["p"][:, d_cols],
                     rhs=z_codes[:].bitcast(FP8X4),
@@ -191,25 +204,10 @@ def tile_nlgate_pa_t_kernel(tc, v, a, Wp, bp, Wg, bg, out_0, out_1):
                 )
                 nc.vector.tensor_scalar(
                     out=phi_bias[:, m, :],
-                    in0=z_phi[:, m, 0:T],
+                    in0=z_phi[:, m, :, 0],
                     scalar1=bp_col[:, m : m + 1],
                     scalar2=None,
                     op0=ADD,
-                )
-
-            for q in range(T // ZZ_STEPS):
-                zz = grouped_pool.tile([P, ZZ_STEPS, P, PACK], BF16, tag="grouped", align_bytes=64)
-                nc.vector.tensor_copy(
-                    out=zz[:],
-                    in_=z_bf16[:, q * ZZ_STEPS : (q + 1) * ZZ_STEPS, :]
-                    .unsqueeze(2)
-                    .to_broadcast([P, ZZ_STEPS, P, PACK]),
-                )
-                zz_cols = slice(q * ZZ_STEPS * P, (q + 1) * ZZ_STEPS * P)
-                nc.vector.quantize_mx(
-                    out=zz_codes[:, zz_cols].bitcast(FP8X4),
-                    scales=zz_scales[:, zz_cols],
-                    in_=zz[:].rearrange("p t c j -> p (t c j)"),
                 )
 
         with tc.psum_pool(name="psum", bufs=4, reuse_waits="tile") as psum:

@@ -26,8 +26,8 @@ D_TILES = D // P
 ROWS = STEP // P
 Z_COPIES = 4
 FIRST_PIECE = 2
-EARLY_STEPS = 4
-VECTOR_COLS = 48
+EARLY_STEPS = 2
+VECTOR_COLS = 64
 
 FLOPS = 2 * 2 * D * PASSES * K_PASS * N
 

@@ -24,9 +24,11 @@ STEP = N // T
 D = 256
 D_TILES = D // P
 ROWS = STEP // P
+G_CHUNKS = (1, 2, 2, 2, 2, 2, 2, 2, 1)
+PHI_CHUNKS = (4, 4, 4, 2, 1, 1)
 Z_COPIES = 4
 FIRST_PIECE = 2
-EARLY_STEPS = 2
+EARLY_STEPS = 0
 VECTOR_COLS = 64
 
 FLOPS = 2 * 2 * D * PASSES * K_PASS * N
@@ -38,13 +40,15 @@ def tile_nlgate_pa_t_kernel(tc, v, a, Wp, bp, Wg, bg, out_0, out_1):
     a_rows = a[0].rearrange("(p j) i f -> p j (i f)", j=PACK)
     v_rows = v[0].rearrange("(p j) t h w -> p j (t h w)", j=PACK)
     phi_out = out_0[0].rearrange("(m p) n -> p m n", p=P)
-    g_out = out_1[0].rearrange("(t c r) d -> t c (r d)", c=P, r=ROWS)
+    g_out = out_1[0].rearrange("(t c r) d -> c t (r d)", c=P, r=ROWS)
 
     with tc.tile_pool(name="resident", bufs=1) as resident, tc.tile_pool(
         name="grouped_pool", bufs=4
     ) as grouped_pool, tc.tile_pool(name="phi_pool", bufs=3) as phi_pool, tc.tile_pool(
-        name="g_pool", bufs=6
-    ) as g_pool:
+        name="g_pool", bufs=5
+    ) as g_pool, tc.tile_pool(name="codes_pool", bufs=4) as codes_pool, tc.manual_schedule(
+        engines={mybir.EngineType.SP}
+    ):
         w_raw = {}
         for name, w in (("p", Wp), ("g", Wg)):
             raw = resident.tile([P, D_TILES, PASSES * K_PASS], BF16, name="w_raw_%s" % name)
@@ -91,8 +95,6 @@ def tile_nlgate_pa_t_kernel(tc, v, a, Wp, bp, Wg, bg, out_0, out_1):
             w_scales[name] = resident.tile(
                 [P, PASSES * D], U8, name="w_scales_%s" % name, align_bytes=64
             )
-        a_codes = resident.tile([P, N], U32, align_bytes=64)
-        a_scales = resident.tile([P, N], U8, align_bytes=64)
         zz_codes = resident.tile([P, T * P], U32, align_bytes=64)
         zz_scales = resident.tile([P, T * P], U8, align_bytes=64)
         z_codes = resident.tile([P, Z_COPIES * T], U32, align_bytes=64)
@@ -215,6 +217,14 @@ def tile_nlgate_pa_t_kernel(tc, v, a, Wp, bp, Wg, bg, out_0, out_1):
             phi_psum_of = {}
             g_psum_of = {}
             phi_stage_of = {}
+            g_stage_of = {}
+            phi_chunk_of = {}
+            g_chunk_of = {}
+            for chunks, chunk_of in ((PHI_CHUNKS, phi_chunk_of), (G_CHUNKS, g_chunk_of)):
+                for steps in chunks:
+                    first = len(chunk_of)
+                    for t in range(first, first + steps):
+                        chunk_of[t] = (first, steps)
 
             def regroup(t):
                 grouped = grouped_pool.tile([P, ROWS, P, PACK], BF16, tag="grouped", align_bytes=64)
@@ -225,10 +235,11 @@ def tile_nlgate_pa_t_kernel(tc, v, a, Wp, bp, Wg, bg, out_0, out_1):
                 grouped_of[t] = grouped
 
             def quantise_and_multiply(t):
-                cols = slice(t * STEP, (t + 1) * STEP)
+                a_codes = codes_pool.tile([P, STEP], U32, align_bytes=64)
+                a_scales = codes_pool.tile([P, STEP], U8, align_bytes=64)
                 nc.vector.quantize_mx(
-                    out=a_codes[:, cols].bitcast(FP8X4),
-                    scales=a_scales[:, cols],
+                    out=a_codes[:].bitcast(FP8X4),
+                    scales=a_scales[:],
                     in_=grouped_of[t][:].rearrange("p r m j -> p (r m j)"),
                 )
                 phi_psum_of[t] = []
@@ -239,8 +250,8 @@ def tile_nlgate_pa_t_kernel(tc, v, a, Wp, bp, Wg, bg, out_0, out_1):
                         out=phi_psum[:],
                         lhsT=w_codes["p"][:, d_cols].bitcast(FP8X4),
                         lhsT_scale=w_scales["p"][:, d_cols],
-                        rhs=a_codes[:, cols].bitcast(FP8X4),
-                        rhs_scale=a_scales[:, cols],
+                        rhs=a_codes[:].bitcast(FP8X4),
+                        rhs_scale=a_scales[:],
                         start=True,
                         stop=True,
                     )
@@ -250,7 +261,7 @@ def tile_nlgate_pa_t_kernel(tc, v, a, Wp, bp, Wg, bg, out_0, out_1):
                     g_psum = psum.tile([P, 2, D], F32)
                     for i in range(2):
                         r = 2 * pair + i
-                        n_cols = slice(t * STEP + r * P, t * STEP + (r + 1) * P)
+                        n_cols = slice(r * P, (r + 1) * P)
                         z_cols_t = slice(t * P, (t + 1) * P)
                         nc.tensor.matmul_mx(
                             out=g_psum[:, i, :],
@@ -273,11 +284,12 @@ def tile_nlgate_pa_t_kernel(tc, v, a, Wp, bp, Wg, bg, out_0, out_1):
                     g_psum_of[t].append(g_psum)
 
             def finish(t):
-                if t % 2 == 0:
-                    phi_stage = phi_pool.tile([P, D_TILES, 2 * STEP], F32)
-                    phi_stage_of[t // 2] = phi_stage
-                phi_stage = phi_stage_of[t // 2]
-                stage_cols = slice((t % 2) * STEP, (t % 2 + 1) * STEP)
+                first, steps = phi_chunk_of[t]
+                if t == first:
+                    phi_stage = phi_pool.tile([P, D_TILES, steps * STEP], F32, tag="phi_stage")
+                    phi_stage_of[first] = phi_stage
+                phi_stage = phi_stage_of[first]
+                stage_cols = slice((t - first) * STEP, (t - first + 1) * STEP)
                 for m in range(D_TILES):
                     nc.scalar.activation(
                         out=phi_stage[:, m, stage_cols].rearrange("p (c r) -> p c r", r=ROWS),
@@ -285,19 +297,27 @@ def tile_nlgate_pa_t_kernel(tc, v, a, Wp, bp, Wg, bg, out_0, out_1):
                         func=IDENTITY,
                         bias=phi_bias[:, m, t : t + 1],
                     )
-                if t % 2 == 1:
+                if t == first + steps - 1:
                     nc.sync.dma_start(
-                        out=phi_out[:, :, (t - 1) * STEP : (t + 1) * STEP], in_=phi_stage[:]
+                        out=phi_out[:, :, first * STEP : (first + steps) * STEP], in_=phi_stage[:]
                     )
-                g_stage = g_pool.tile([P, ROWS, D], F32)
+                first, steps = g_chunk_of[t]
+                if t == first:
+                    g_stage = g_pool.tile([P, steps, ROWS, D], F32, tag="g_stage")
+                    g_stage_of[first] = g_stage
+                g_stage = g_stage_of[first]
                 for pair in range(ROWS // 2):
                     nc.vector.tensor_tensor(
-                        out=g_stage[:, 2 * pair : 2 * pair + 2, :],
+                        out=g_stage[:, t - first, 2 * pair : 2 * pair + 2, :],
                         in0=g_psum_of[t][pair][:],
                         in1=bg_all[:].unsqueeze(1).to_broadcast([P, 2, D]),
                         op=ADD,
                     )
-                nc.sync.dma_start(out=g_out[t], in_=g_stage[:].rearrange("p r d -> p (r d)"))
+                if t == first + steps - 1:
+                    nc.sync.dma_start(
+                        out=g_out[:, first : first + steps, :],
+                        in_=g_stage[:].rearrange("p t r d -> p t (r d)"),
+                    )
 
             for t in range(-2, T):
                 if t + 2 < T:

@@ -25,7 +25,7 @@ D = 256
 D_TILES = D // P
 ROWS = STEP // P
 G_CHUNKS = (1, 2, 2, 2, 2, 2, 2, 2, 1)
-PHI_CHUNKS = (4, 4, 4, 2, 1, 1)
+PHI_CHUNKS = (2, 2, 2, 2, 2, 2, 2, 2)
 Z_COPIES = 4
 FIRST_PIECE = 2
 EARLY_STEPS = 0
@@ -44,7 +44,7 @@ def tile_nlgate_pa_t_kernel(tc, v, a, Wp, bp, Wg, bg, out_0, out_1):
 
     with tc.tile_pool(name="resident", bufs=1) as resident, tc.tile_pool(
         name="grouped_pool", bufs=4
-    ) as grouped_pool, tc.tile_pool(name="phi_pool", bufs=3) as phi_pool, tc.tile_pool(
+    ) as grouped_pool, tc.tile_pool(name="phi_pool", bufs=5) as phi_pool, tc.tile_pool(
         name="g_pool", bufs=5
     ) as g_pool, tc.tile_pool(name="codes_pool", bufs=4) as codes_pool, tc.manual_schedule(
         engines={mybir.EngineType.SP}

@@ -25,7 +25,7 @@ D = 256
 D_TILES = D // P
 ROWS = STEP // P
 G_CHUNKS = (1, 2, 2, 2, 2, 2, 2, 2, 1)
-PHI_CHUNKS = (2, 2, 2, 2, 2, 2, 2, 2)
+PHI_CHUNKS = (2, 2, 4, 4, 4)
 Z_COPIES = 4
 FIRST_PIECE = 2
 EARLY_STEPS = 0
@@ -44,7 +44,7 @@ def tile_nlgate_pa_t_kernel(tc, v, a, Wp, bp, Wg, bg, out_0, out_1):
 
     with tc.tile_pool(name="resident", bufs=1) as resident, tc.tile_pool(
         name="grouped_pool", bufs=4
-    ) as grouped_pool, tc.tile_pool(name="phi_pool", bufs=5) as phi_pool, tc.tile_pool(
+    ) as grouped_pool, tc.tile_pool(name="phi_pool", bufs=3) as phi_pool, tc.tile_pool(
         name="g_pool", bufs=5
     ) as g_pool, tc.tile_pool(name="codes_pool", bufs=4) as codes_pool, tc.manual_schedule(
         engines={mybir.EngineType.SP}

@@ -24,7 +24,7 @@ STEP = N // T
 D = 256
 D_TILES = D // P
 ROWS = STEP // P
-G_CHUNKS = (1, 2, 2, 2, 2, 2, 2, 2, 1)
+G_CHUNKS = (1, 2, 3, 4, 4, 1, 1)
 PHI_CHUNKS = (2, 2, 4, 4, 4)
 Z_COPIES = 4
 FIRST_PIECE = 2
@@ -45,174 +45,175 @@ def tile_nlgate_pa_t_kernel(tc, v, a, Wp, bp, Wg, bg, out_0, out_1):
     with tc.tile_pool(name="resident", bufs=1) as resident, tc.tile_pool(
         name="grouped_pool", bufs=4
     ) as grouped_pool, tc.tile_pool(name="phi_pool", bufs=3) as phi_pool, tc.tile_pool(
-        name="g_pool", bufs=5
-    ) as g_pool, tc.tile_pool(name="codes_pool", bufs=4) as codes_pool, tc.manual_schedule(
-        engines={mybir.EngineType.SP}
-    ):
-        w_raw = {}
-        for name, w in (("p", Wp), ("g", Wg)):
-            raw = resident.tile([P, D_TILES, PASSES * K_PASS], BF16, name="w_raw_%s" % name)
-            nc.sync.dma_start(out=raw[:], in_=w.rearrange("(m p) k -> p m k", p=P))
-            w_raw[name] = raw
+        name="codes_pool", bufs=4
+    ) as codes_pool, tc.manual_schedule(engines={mybir.EngineType.SP}):
+        with tc.tile_pool(name="load_pool", bufs=1) as load_pool:
+            w_raw = {}
+            for name, w in (("p", Wp), ("g", Wg)):
+                raw = load_pool.tile([P, D_TILES, PASSES * K_PASS], BF16, name="w_raw_%s" % name)
+                nc.sync.dma_start(out=raw[:], in_=w.rearrange("(m p) k -> p m k", p=P))
+                w_raw[name] = raw
 
-        def load_v_and_biases():
-            for j in range(PACK):
-                nc.sync.dma_start(out=v_raw[:, j, :], in_=v_rows[:, j, :])
-            nc.sync.dma_start(out=bias_rows[0:1, 0:D], in_=bp.unsqueeze(0))
-            nc.sync.dma_start(out=bias_rows[0:1, D : 2 * D], in_=bg.unsqueeze(0))
+            def load_v_and_biases():
+                for j in range(PACK):
+                    nc.sync.dma_start(out=v_raw[:, j, :], in_=v_rows[:, j, :])
+                nc.sync.dma_start(out=bias_rows[0:1, 0:D], in_=bp.unsqueeze(0))
+                nc.sync.dma_start(out=bias_rows[0:1, D : 2 * D], in_=bg.unsqueeze(0))
 
-        v_raw = resident.tile([P, PACK, T * H * W], BF16)
-        bias_rows = resident.tile([P, 2 * D], BF16)
-        nc.vector.memset(bias_rows[:], 0.0)
+            v_raw = load_pool.tile([P, PACK, T * H * W], BF16)
+            bias_rows = load_pool.tile([P, 2 * D], BF16)
+            nc.vector.memset(bias_rows[:], 0.0)
 
-        a_step = []
-        piece_steps = FIRST_PIECE
-        while len(a_step) < T:
-            if len(a_step) == EARLY_STEPS:
-                load_v_and_biases()
-            first = len(a_step)
-            raw = resident.tile([P, PACK, piece_steps * STEP], BF16, name="a_raw_%d" % first)
-            nc.sync.dma_start(
-                out=raw[:], in_=a_rows[:, :, first * STEP : (first + piece_steps) * STEP]
-            )
-            for s in range(piece_steps):
-                a_step.append(raw[:, :, s * STEP : (s + 1) * STEP])
-            piece_steps = len(a_step)
+            a_step = []
+            piece_steps = FIRST_PIECE
+            while len(a_step) < T:
+                if len(a_step) == EARLY_STEPS:
+                    load_v_and_biases()
+                first = len(a_step)
+                raw = resident.tile([P, PACK, piece_steps * STEP], BF16, name="a_raw_%d" % first)
+                nc.sync.dma_start(
+                    out=raw[:], in_=a_rows[:, :, first * STEP : (first + piece_steps) * STEP]
+                )
+                for s in range(piece_steps):
+                    a_step.append(raw[:, :, s * STEP : (s + 1) * STEP])
+                piece_steps = len(a_step)
 
-        ones = resident.tile([P, P], BF16)
-        nc.vector.memset(ones[:], 1.0)
-        ident_bf16 = resident.tile([P, P], BF16)
-        make_identity(nc, ident_bf16[:])
-        ident_f32 = resident.tile([P, P], F32)
-        make_identity(nc, ident_f32[:])
+            ones = resident.tile([P, P], BF16)
+            nc.vector.memset(ones[:], 1.0)
+            ident_bf16 = resident.tile([P, P], BF16)
+            make_identity(nc, ident_bf16[:])
+            ident_f32 = resident.tile([P, P], F32)
+            make_identity(nc, ident_f32[:])
 
-        w_codes = {}
-        w_scales = {}
-        for name in ("p", "g"):
-            w_codes[name] = resident.tile(
-                [P, PASSES * D], U32, name="w_codes_%s" % name, align_bytes=64
-            )
-            w_scales[name] = resident.tile(
-                [P, PASSES * D], U8, name="w_scales_%s" % name, align_bytes=64
-            )
-        zz_codes = resident.tile([P, T * P], U32, align_bytes=64)
-        zz_scales = resident.tile([P, T * P], U8, align_bytes=64)
-        z_codes = resident.tile([P, Z_COPIES * T], U32, align_bytes=64)
-        z_scales = resident.tile([P, Z_COPIES * T], U8, align_bytes=64)
-
-        bg_all = resident.tile([P, D], F32)
-        bp_col = resident.tile([P, D_TILES], F32)
-        phi_bias = resident.tile([P, D_TILES, T], F32)
-        z_sum = resident.tile([P, PACK, T], F32)
-
-        with tc.psum_pool(name="setup_psum", bufs=1) as setup_psum:
+            w_codes = {}
+            w_scales = {}
             for name in ("p", "g"):
-                words = w_raw[name][:].bitcast(F32).rearrange(
-                    "p m (g q u) -> p m g u q", g=PASSES, u=2
+                w_codes[name] = resident.tile(
+                    [P, PASSES * D], U32, name="w_codes_%s" % name, align_bytes=64
                 )
-                w_grouped = grouped_pool.tile(
-                    [P, PASSES, D_TILES, P, PACK], BF16, tag="grouped", align_bytes=64
+                w_scales[name] = resident.tile(
+                    [P, PASSES * D], U8, name="w_scales_%s" % name, align_bytes=64
                 )
-                for g in range(PASSES):
-                    w_t = setup_psum.tile([P, D_TILES, 2, P], F32, tag="w_t", bufs=4)
-                    for m in range(D_TILES):
-                        for u in range(2):
-                            nc.tensor.transpose(w_t[:, m, u, :], words[:, m, g, u, :], ident_f32[:])
-                    grouped_words = w_grouped[:, g].bitcast(F32)
-                    if g == 0:
-                        nc.vector.tensor_copy(
-                            out=grouped_words, in_=w_t[:].rearrange("p m u d -> p m d u")
-                        )
-                    else:
-                        nc.scalar.copy(out=grouped_words, in_=w_t[:].rearrange("p m u d -> p m d u"))
-                nc.vector.quantize_mx(
-                    out=w_codes[name][:].bitcast(FP8X4),
-                    scales=w_scales[name][:],
-                    in_=w_grouped[:].rearrange("p g m d j -> p (g m d j)"),
-                )
+            zz_codes = resident.tile([P, T * P], U32, align_bytes=64)
+            zz_scales = resident.tile([P, T * P], U8, align_bytes=64)
+            z_codes = resident.tile([P, Z_COPIES * T], U32, align_bytes=64)
+            z_scales = resident.tile([P, Z_COPIES * T], U8, align_bytes=64)
 
-            frames = v_raw[:].rearrange("p j (t h w) -> p j t h w", h=H, w=W)
-            for half in range(2):
-                row_sum = setup_psum.tile([P, 2, T, W], F32, tag="row_sum", bufs=2)
-                for i in range(2):
-                    for h in range(H):
-                        nc.tensor.matmul(
-                            out=row_sum[:, i],
-                            lhsT=ident_bf16[:],
-                            rhs=frames[:, 2 * half + i, :, h, :],
-                            start=(h == 0),
-                            stop=(h == H - 1),
-                        )
-                nc.vector.tensor_reduce(
-                    out=z_sum[:, 2 * half : 2 * half + 2, :], in_=row_sum[:], axis=AXIS_X, op=ADD
-                )
-            z_cols = resident.tile([P, T, Z_COPIES, PACK], BF16, align_bytes=64)
-            nc.vector.tensor_scalar(
-                out=z_cols[:],
-                in0=z_sum[:].rearrange("p j t -> p t j").unsqueeze(2).to_broadcast([P, T, Z_COPIES, PACK]),
-                scalar1=1.0 / (H * W),
-                scalar2=None,
-                op0=MULT,
-            )
-            nc.vector.memset(z_scales[:].bitcast(I32), 0)
-            nc.vector.quantize_mx(
-                out=z_codes[:].bitcast(FP8X4),
-                scales=z_scales[:],
-                in_=z_cols[:].rearrange("p t c j -> p (t c j)"),
-            )
+            bg_all = resident.tile([P, D], F32)
+            bp_col = resident.tile([P, D_TILES], F32)
+            phi_bias = resident.tile([P, D_TILES, T], F32)
+            z_sum = resident.tile([P, PACK, T], F32)
 
-            bias_psum = setup_psum.tile([P, 2 * D], F32)
-            nc.tensor.matmul(
-                out=bias_psum[:, 0:D], lhsT=ones[:], rhs=bias_rows[:, D : 2 * D], start=True, stop=True
-            )
-            for m in range(D_TILES):
-                nc.tensor.matmul(
-                    out=bias_psum[:, D + 32 * m : D + 32 * (m + 1)],
-                    lhsT=bias_rows[:, m * P : (m + 1) * P],
-                    rhs=ones[:, 0:32],
-                    start=True,
-                    stop=True,
-                )
-            nc.vector.tensor_copy(out=bg_all[:], in_=bias_psum[:, 0:D])
-            nc.vector.tensor_copy(
-                out=bp_col[:],
-                in_=bias_psum[:, D : D + 32 * D_TILES].rearrange("p (m n) -> p m n", n=32)[:, :, 0],
-            )
+            with tc.psum_pool(name="setup_psum", bufs=1) as setup_psum:
+                for name in ("p", "g"):
+                    words = w_raw[name][:].bitcast(F32).rearrange(
+                        "p m (g q u) -> p m g u q", g=PASSES, u=2
+                    )
+                    w_grouped = grouped_pool.tile(
+                        [P, PASSES, D_TILES, P, PACK], BF16, tag="grouped", align_bytes=64
+                    )
+                    for g in range(PASSES):
+                        w_t = setup_psum.tile([P, D_TILES, 2, P], F32, tag="w_t", bufs=4)
+                        for m in range(D_TILES):
+                            for u in range(2):
+                                nc.tensor.transpose(w_t[:, m, u, :], words[:, m, g, u, :], ident_f32[:])
+                        grouped_words = w_grouped[:, g].bitcast(F32)
+                        if g == 0:
+                            nc.vector.tensor_copy(
+                                out=grouped_words, in_=w_t[:].rearrange("p m u d -> p m d u")
+                            )
+                        else:
+                            nc.scalar.copy(out=grouped_words, in_=w_t[:].rearrange("p m u d -> p m d u"))
+                    nc.vector.quantize_mx(
+                        out=w_codes[name][:].bitcast(FP8X4),
+                        scales=w_scales[name][:],
+                        in_=w_grouped[:].rearrange("p g m d j -> p (g m d j)"),
+                    )
 
-            nc.vector.tensor_copy(
-                out=zz_codes[:].bitcast(I32).rearrange("p (t b c) -> p t b c", t=T, c=Z_COPIES),
-                in_=z_codes[:]
-                .bitcast(I32)
-                .rearrange("p (t c) -> p t c", c=Z_COPIES)
-                .unsqueeze(2)
-                .to_broadcast([P, T, P // Z_COPIES, Z_COPIES]),
-            )
-            nc.vector.tensor_copy(
-                out=zz_scales[:].bitcast(I32).rearrange("p (t b) -> p t b", t=T),
-                in_=z_scales[:].bitcast(I32).unsqueeze(2).to_broadcast([P, T, P // Z_COPIES]),
-            )
-
-            z_phi = setup_psum.tile([P, D_TILES, T, Z_COPIES], F32)
-            for m in range(D_TILES):
-                d_cols = slice(D + m * P, D + (m + 1) * P)
-                nc.tensor.matmul_mx(
-                    out=z_phi[:, m],
-                    lhsT=w_codes["p"][:, d_cols].bitcast(FP8X4),
-                    lhsT_scale=w_scales["p"][:, d_cols],
-                    rhs=z_codes[:].bitcast(FP8X4),
-                    rhs_scale=z_scales[:],
-                    start=True,
-                    stop=True,
-                )
+                frames = v_raw[:].rearrange("p j (t h w) -> p j t h w", h=H, w=W)
+                for half in range(2):
+                    row_sum = setup_psum.tile([P, 2, T, W], F32, tag="row_sum", bufs=2)
+                    for i in range(2):
+                        for h in range(H):
+                            nc.tensor.matmul(
+                                out=row_sum[:, i],
+                                lhsT=ident_bf16[:],
+                                rhs=frames[:, 2 * half + i, :, h, :],
+                                start=(h == 0),
+                                stop=(h == H - 1),
+                            )
+                    nc.vector.tensor_reduce(
+                        out=z_sum[:, 2 * half : 2 * half + 2, :], in_=row_sum[:], axis=AXIS_X, op=ADD
+                    )
+                z_cols = resident.tile([P, T, Z_COPIES, PACK], BF16, align_bytes=64)
                 nc.vector.tensor_scalar(
-                    out=phi_bias[:, m, :],
-                    in0=z_phi[:, m, :, 0],
-                    scalar1=bp_col[:, m : m + 1],
+                    out=z_cols[:],
+                    in0=z_sum[:].rearrange("p j t -> p t j").unsqueeze(2).to_broadcast([P, T, Z_COPIES, PACK]),
+                    scalar1=1.0 / (H * W),
                     scalar2=None,
-                    op0=ADD,
+                    op0=MULT,
+                )
+                nc.vector.memset(z_scales[:].bitcast(I32), 0)
+                nc.vector.quantize_mx(
+                    out=z_codes[:].bitcast(FP8X4),
+                    scales=z_scales[:],
+                    in_=z_cols[:].rearrange("p t c j -> p (t c j)"),
                 )
 
-        with tc.psum_pool(name="psum", bufs=4, reuse_waits="tile") as psum:
+                bias_psum = setup_psum.tile([P, 2 * D], F32)
+                nc.tensor.matmul(
+                    out=bias_psum[:, 0:D], lhsT=ones[:], rhs=bias_rows[:, D : 2 * D], start=True, stop=True
+                )
+                for m in range(D_TILES):
+                    nc.tensor.matmul(
+                        out=bias_psum[:, D + 32 * m : D + 32 * (m + 1)],
+                        lhsT=bias_rows[:, m * P : (m + 1) * P],
+                        rhs=ones[:, 0:32],
+                        start=True,
+                        stop=True,
+                    )
+                nc.vector.tensor_copy(out=bg_all[:], in_=bias_psum[:, 0:D])
+                nc.vector.tensor_copy(
+                    out=bp_col[:],
+                    in_=bias_psum[:, D : D + 32 * D_TILES].rearrange("p (m n) -> p m n", n=32)[:, :, 0],
+                )
+
+                nc.vector.tensor_copy(
+                    out=zz_codes[:].bitcast(I32).rearrange("p (t b c) -> p t b c", t=T, c=Z_COPIES),
+                    in_=z_codes[:]
+                    .bitcast(I32)
+                    .rearrange("p (t c) -> p t c", c=Z_COPIES)
+                    .unsqueeze(2)
+                    .to_broadcast([P, T, P // Z_COPIES, Z_COPIES]),
+                )
+                nc.vector.tensor_copy(
+                    out=zz_scales[:].bitcast(I32).rearrange("p (t b) -> p t b", t=T),
+                    in_=z_scales[:].bitcast(I32).unsqueeze(2).to_broadcast([P, T, P // Z_COPIES]),
+                )
+
+                z_phi = setup_psum.tile([P, D_TILES, T, Z_COPIES], F32)
+                for m in range(D_TILES):
+                    d_cols = slice(D + m * P, D + (m + 1) * P)
+                    nc.tensor.matmul_mx(
+                        out=z_phi[:, m],
+                        lhsT=w_codes["p"][:, d_cols].bitcast(FP8X4),
+                        lhsT_scale=w_scales["p"][:, d_cols],
+                        rhs=z_codes[:].bitcast(FP8X4),
+                        rhs_scale=z_scales[:],
+                        start=True,
+                        stop=True,
+                    )
+                    nc.vector.tensor_scalar(
+                        out=phi_bias[:, m, :],
+                        in0=z_phi[:, m, :, 0],
+                        scalar1=bp_col[:, m : m + 1],
+                        scalar2=None,
+                        op0=ADD,
+                    )
+
+        with tc.tile_pool(name="g_pool", bufs=4) as g_pool, tc.psum_pool(
+            name="psum", bufs=4, reuse_waits="tile"
+        ) as psum:
             grouped_of = {}
             phi_psum_of = {}
             g_psum_of = {}

@@ -24,7 +24,7 @@ STEP = N // T
 D = 256
 D_TILES = D // P
 ROWS = STEP // P
-G_CHUNKS = (1, 2, 3, 4, 4, 1, 1)
+G_CHUNKS = (3, 3, 4, 4, 2)
 PHI_CHUNKS = (2, 2, 4, 4, 4)
 Z_COPIES = 4
 FIRST_PIECE = 2
@@ -55,8 +55,10 @@ def tile_nlgate_pa_t_kernel(tc, v, a, Wp, bp, Wg, bg, out_0, out_1):
                 w_raw[name] = raw
 
             def load_v_and_biases():
-                for j in range(PACK):
-                    nc.sync.dma_start(out=v_raw[:, j, :], in_=v_rows[:, j, :])
+                for half in range(2):
+                    nc.sync.dma_start(
+                        out=v_raw[:, 2 * half : 2 * half + 2, :], in_=v_rows[:, 2 * half : 2 * half + 2, :]
+                    )
                 nc.sync.dma_start(out=bias_rows[0:1, 0:D], in_=bp.unsqueeze(0))
                 nc.sync.dma_start(out=bias_rows[0:1, D : 2 * D], in_=bg.unsqueeze(0))
 

@@ -24,7 +24,7 @@ STEP = N // T
 D = 256
 D_TILES = D // P
 ROWS = STEP // P
-G_CHUNKS = (3, 3, 4, 4, 2)
+G_CHUNKS = (3, 3, 4, 4, 1, 1)
 PHI_CHUNKS = (2, 2, 4, 4, 4)
 Z_COPIES = 4
 FIRST_PIECE = 2

@@ -29,6 +29,7 @@ PHI_CHUNKS = (2, 2, 4, 4, 4)
 Z_COPIES = 4
 FIRST_PIECE = 2
 EARLY_STEPS = 0
+DMA_ALIGN = 256
 VECTOR_COLS = 64
 
 FLOPS = 2 * 2 * D * PASSES * K_PASS * N
@@ -50,7 +51,9 @@ def tile_nlgate_pa_t_kernel(tc, v, a, Wp, bp, Wg, bg, out_0, out_1):
         with tc.tile_pool(name="load_pool", bufs=1) as load_pool:
             w_raw = {}
             for name, w in (("p", Wp), ("g", Wg)):
-                raw = load_pool.tile([P, D_TILES, PASSES * K_PASS], BF16, name="w_raw_%s" % name)
+                raw = load_pool.tile(
+                    [P, D_TILES, PASSES * K_PASS], BF16, name="w_raw_%s" % name, align_bytes=DMA_ALIGN
+                )
                 nc.sync.dma_start(out=raw[:], in_=w.rearrange("(m p) k -> p m k", p=P))
                 w_raw[name] = raw
 
@@ -62,7 +65,7 @@ def tile_nlgate_pa_t_kernel(tc, v, a, Wp, bp, Wg, bg, out_0, out_1):
                 nc.sync.dma_start(out=bias_rows[0:1, 0:D], in_=bp.unsqueeze(0))
                 nc.sync.dma_start(out=bias_rows[0:1, D : 2 * D], in_=bg.unsqueeze(0))
 
-            v_raw = load_pool.tile([P, PACK, T * H * W], BF16)
+            v_raw = load_pool.tile([P, PACK, T * H * W], BF16, align_bytes=DMA_ALIGN)
             bias_rows = load_pool.tile([P, 2 * D], BF16)
             nc.vector.memset(bias_rows[:], 0.0)
 
@@ -72,7 +75,9 @@ def tile_nlgate_pa_t_kernel(tc, v, a, Wp, bp, Wg, bg, out_0, out_1):
                 if len(a_step) == EARLY_STEPS:
                     load_v_and_biases()
                 first = len(a_step)
-                raw = resident.tile([P, PACK, piece_steps * STEP], BF16, name="a_raw_%d" % first)
+                raw = resident.tile(
+                    [P, PACK, piece_steps * STEP], BF16, name="a_raw_%d" % first, align_bytes=DMA_ALIGN
+                )
                 nc.sync.dma_start(
                     out=raw[:], in_=a_rows[:, :, first * STEP : (first + piece_steps) * STEP]
                 )
@@ -289,7 +294,9 @@ def tile_nlgate_pa_t_kernel(tc, v, a, Wp, bp, Wg, bg, out_0, out_1):
             def finish(t):
                 first, steps = phi_chunk_of[t]
                 if t == first:
-                    phi_stage = phi_pool.tile([P, D_TILES, steps * STEP], F32, tag="phi_stage")
+                    phi_stage = phi_pool.tile(
+                        [P, D_TILES, steps * STEP], F32, tag="phi_stage", align_bytes=DMA_ALIGN
+                    )
                     phi_stage_of[first] = phi_stage
                 phi_stage = phi_stage_of[first]
                 stage_cols = slice((t - first) * STEP, (t - first + 1) * STEP)
@@ -306,7 +313,9 @@ def tile_nlgate_pa_t_kernel(tc, v, a, Wp, bp, Wg, bg, out_0, out_1):
                     )
                 first, steps = g_chunk_of[t]
                 if t == first:
-                    g_stage = g_pool.tile([P, steps, ROWS, D], F32, tag="g_stage")
+                    g_stage = g_pool.tile(
+                        [P, steps, ROWS, D], F32, tag="g_stage", align_bytes=DMA_ALIGN
+                    )
                     g_stage_of[first] = g_stage
                 g_stage = g_stage_of[first]
                 for pair in range(ROWS // 2):

@@ -11,6 +11,12 @@ ADD = mybir.AluOpType.add
 MULT = mybir.AluOpType.mult
 IDENTITY = mybir.ActivationFunctionType.Identity
 AXIS_X = mybir.AxisListType.X
+ORDERED = {
+    mybir.EngineType.SP,
+    mybir.EngineType.PE,
+    mybir.EngineType.DVE,
+    mybir.EngineType.Activation,
+}
 
 P = 128
 PACK = 4
@@ -24,11 +30,11 @@ STEP = N // T
 D = 256
 D_TILES = D // P
 ROWS = STEP // P
-G_CHUNKS = (3, 3, 4, 4, 1, 1)
-PHI_CHUNKS = (2, 2, 4, 4, 4)
+G_CHUNKS = (3, 3, 3, 3, 3, 1)
+PHI_CHUNKS = (2, 3, 3, 3, 3, 2)
+A_PIECES = (2, 2, 4, 8)
 Z_COPIES = 4
-FIRST_PIECE = 2
-EARLY_STEPS = 0
+ZZ_PARTS = (4, 12)
 DMA_ALIGN = 256
 VECTOR_COLS = 64
 
@@ -45,10 +51,115 @@ def tile_nlgate_pa_t_kernel(tc, v, a, Wp, bp, Wg, bg, out_0, out_1):
 
     with tc.tile_pool(name="resident", bufs=1) as resident, tc.tile_pool(
         name="grouped_pool", bufs=4
-    ) as grouped_pool, tc.tile_pool(name="phi_pool", bufs=3) as phi_pool, tc.tile_pool(
+    ) as grouped_pool, tc.tile_pool(name="phi_pool", bufs=4) as phi_pool, tc.tile_pool(
         name="codes_pool", bufs=4
-    ) as codes_pool, tc.manual_schedule(engines={mybir.EngineType.SP}):
+    ) as codes_pool, tc.psum_pool(
+        name="psum", bufs=4, reuse_waits="tile"
+    ) as psum, tc.manual_schedule(engines=ORDERED):
+        grouped_of = {}
+        a_codes_of = {}
+        phi_psum_of = {}
+        g_psum_of = {}
+        phi_stage_of = {}
+        g_stage_of = {}
+        phi_chunk_of = {}
+        g_chunk_of = {}
+        for chunks, chunk_of in ((PHI_CHUNKS, phi_chunk_of), (G_CHUNKS, g_chunk_of)):
+            for steps in chunks:
+                first = len(chunk_of)
+                for t in range(first, first + steps):
+                    chunk_of[t] = (first, steps)
+
+        w_codes = {}
+        w_scales = {}
+        for name in ("p", "g"):
+            w_codes[name] = resident.tile([P, PASSES * D], U32, name="w_codes_%s" % name, align_bytes=64)
+            w_scales[name] = resident.tile([P, PASSES * D], U8, name="w_scales_%s" % name, align_bytes=64)
+        zz_codes = resident.tile([P, T * P], U32, align_bytes=64)
+        zz_scales = resident.tile([P, T * P], U8, align_bytes=64)
+        z_codes = resident.tile([P, Z_COPIES * T], U32, align_bytes=64)
+        z_scales = resident.tile([P, Z_COPIES * T], U8, align_bytes=64)
+        z_cols = resident.tile([P, T, Z_COPIES, PACK], BF16, align_bytes=64)
+        z_sum = resident.tile([P, PACK, T], F32)
+        bg_all = resident.tile([P, D], F32)
+        bp_col = resident.tile([P, D_TILES], F32)
+        phi_bias = resident.tile([P, D_TILES, T], F32)
+        ones = resident.tile([P, P], BF16)
+        ident_bf16 = resident.tile([P, P], BF16)
+        ident_f32 = resident.tile([P, P], F32)
+
+        def regroup(t):
+            grouped = grouped_pool.tile([P, ROWS, P, PACK], BF16, tag="grouped", align_bytes=64)
+            dst = grouped[:].rearrange("p r m j -> p m j r")
+            src = a_step[t].rearrange("p j (m r) -> p m j r", r=ROWS)
+            nc.vector.tensor_copy(out=dst[:, 0:VECTOR_COLS], in_=src[:, 0:VECTOR_COLS])
+            nc.scalar.copy(out=dst[:, VECTOR_COLS:P], in_=src[:, VECTOR_COLS:P])
+            grouped_of[t] = grouped
+
+        def quantise(t):
+            a_codes = codes_pool.tile([P, STEP], U32, align_bytes=64)
+            a_scales = codes_pool.tile([P, STEP], U8, align_bytes=64)
+            nc.vector.quantize_mx(
+                out=a_codes[:].bitcast(FP8X4),
+                scales=a_scales[:],
+                in_=grouped_of[t][:].rearrange("p r m j -> p (r m j)"),
+            )
+            a_codes_of[t] = (a_codes, a_scales)
+
+        def multiply_phi(t):
+            a_codes, a_scales = a_codes_of[t]
+            phi_psum_of[t] = []
+            for m in range(D_TILES):
+                phi_psum = psum.tile([P, STEP], F32, tag="phi_psum")
+                d_cols = slice(m * P, (m + 1) * P)
+                nc.tensor.matmul_mx(
+                    out=phi_psum[:],
+                    lhsT=w_codes["p"][:, d_cols].bitcast(FP8X4),
+                    lhsT_scale=w_scales["p"][:, d_cols],
+                    rhs=a_codes[:].bitcast(FP8X4),
+                    rhs_scale=a_scales[:],
+                    start=True,
+                    stop=True,
+                )
+                phi_psum_of[t].append(phi_psum)
+
+        def multiply_g(t):
+            a_codes, a_scales = a_codes_of[t]
+            z_cols_t = slice(t * P, (t + 1) * P)
+            g_psum_of[t] = []
+            for pair in range(ROWS // 2):
+                g_psum = psum.tile([P, 2, D], F32, tag="g_psum")
+                for i in range(2):
+                    r = 2 * pair + i
+                    n_cols = slice(r * P, (r + 1) * P)
+                    nc.tensor.matmul_mx(
+                        out=g_psum[:, i, :],
+                        lhsT=a_codes[:, n_cols].bitcast(FP8X4),
+                        lhsT_scale=a_scales[:, n_cols],
+                        rhs=w_codes["g"][:, 0:D].bitcast(FP8X4),
+                        rhs_scale=w_scales["g"][:, 0:D],
+                        start=True,
+                        stop=False,
+                    )
+                    nc.tensor.matmul_mx(
+                        out=g_psum[:, i, :],
+                        lhsT=zz_codes[:, z_cols_t].bitcast(FP8X4),
+                        lhsT_scale=zz_scales[:, z_cols_t],
+                        rhs=w_codes["g"][:, D : 2 * D].bitcast(FP8X4),
+                        rhs_scale=w_scales["g"][:, D : 2 * D],
+                        start=False,
+                        stop=True,
+                    )
+                g_psum_of[t].append(g_psum)
+
         with tc.tile_pool(name="load_pool", bufs=1) as load_pool:
+            bias_rows = load_pool.tile([P, 2 * D], BF16)
+            nc.vector.memset(bias_rows[:], 0.0)
+            nc.vector.memset(ones[:], 1.0)
+            nc.vector.memset(z_scales[:].bitcast(I32), 0)
+            make_identity(nc, ident_f32[:])
+            make_identity(nc, ident_bf16[:])
+
             w_raw = {}
             for name, w in (("p", Wp), ("g", Wg)):
                 raw = load_pool.tile(
@@ -56,24 +167,15 @@ def tile_nlgate_pa_t_kernel(tc, v, a, Wp, bp, Wg, bg, out_0, out_1):
                 )
                 nc.sync.dma_start(out=raw[:], in_=w.rearrange("(m p) k -> p m k", p=P))
                 w_raw[name] = raw
-
-            def load_v_and_biases():
-                for half in range(2):
-                    nc.sync.dma_start(
-                        out=v_raw[:, 2 * half : 2 * half + 2, :], in_=v_rows[:, 2 * half : 2 * half + 2, :]
-                    )
-                nc.sync.dma_start(out=bias_rows[0:1, 0:D], in_=bp.unsqueeze(0))
-                nc.sync.dma_start(out=bias_rows[0:1, D : 2 * D], in_=bg.unsqueeze(0))
-
             v_raw = load_pool.tile([P, PACK, T * H * W], BF16, align_bytes=DMA_ALIGN)
-            bias_rows = load_pool.tile([P, 2 * D], BF16)
-            nc.vector.memset(bias_rows[:], 0.0)
-
+            for half in range(2):
+                nc.sync.dma_start(
+                    out=v_raw[:, 2 * half : 2 * half + 2, :], in_=v_rows[:, 2 * half : 2 * half + 2, :]
+                )
+            nc.sync.dma_start(out=bias_rows[0:1, 0:D], in_=bp.unsqueeze(0))
+            nc.sync.dma_start(out=bias_rows[0:1, D : 2 * D], in_=bg.unsqueeze(0))
             a_step = []
-            piece_steps = FIRST_PIECE
-            while len(a_step) < T:
-                if len(a_step) == EARLY_STEPS:
-                    load_v_and_biases()
+            for piece_steps in A_PIECES:
                 first = len(a_step)
                 raw = resident.tile(
                     [P, PACK, piece_steps * STEP], BF16, name="a_raw_%d" % first, align_bytes=DMA_ALIGN
@@ -83,213 +185,121 @@ def tile_nlgate_pa_t_kernel(tc, v, a, Wp, bp, Wg, bg, out_0, out_1):
                 )
                 for s in range(piece_steps):
                     a_step.append(raw[:, :, s * STEP : (s + 1) * STEP])
-                piece_steps = len(a_step)
 
-            ones = resident.tile([P, P], BF16)
-            nc.vector.memset(ones[:], 1.0)
-            ident_bf16 = resident.tile([P, P], BF16)
-            make_identity(nc, ident_bf16[:])
-            ident_f32 = resident.tile([P, P], F32)
-            make_identity(nc, ident_f32[:])
-
-            w_codes = {}
-            w_scales = {}
+            w_grouped = {}
             for name in ("p", "g"):
-                w_codes[name] = resident.tile(
-                    [P, PASSES * D], U32, name="w_codes_%s" % name, align_bytes=64
+                words = w_raw[name][:].bitcast(F32).rearrange("p m (g q u) -> p m g u q", g=PASSES, u=2)
+                w_grouped[name] = grouped_pool.tile(
+                    [P, PASSES, D_TILES, P, PACK], BF16, name="w_grouped_%s" % name, tag="grouped", align_bytes=64
                 )
-                w_scales[name] = resident.tile(
-                    [P, PASSES * D], U8, name="w_scales_%s" % name, align_bytes=64
-                )
-            zz_codes = resident.tile([P, T * P], U32, align_bytes=64)
-            zz_scales = resident.tile([P, T * P], U8, align_bytes=64)
-            z_codes = resident.tile([P, Z_COPIES * T], U32, align_bytes=64)
-            z_scales = resident.tile([P, Z_COPIES * T], U8, align_bytes=64)
-
-            bg_all = resident.tile([P, D], F32)
-            bp_col = resident.tile([P, D_TILES], F32)
-            phi_bias = resident.tile([P, D_TILES, T], F32)
-            z_sum = resident.tile([P, PACK, T], F32)
-
-            with tc.psum_pool(name="setup_psum", bufs=1) as setup_psum:
-                for name in ("p", "g"):
-                    words = w_raw[name][:].bitcast(F32).rearrange(
-                        "p m (g q u) -> p m g u q", g=PASSES, u=2
-                    )
-                    w_grouped = grouped_pool.tile(
-                        [P, PASSES, D_TILES, P, PACK], BF16, tag="grouped", align_bytes=64
-                    )
-                    for g in range(PASSES):
-                        w_t = setup_psum.tile([P, D_TILES, 2, P], F32, tag="w_t", bufs=4)
-                        for m in range(D_TILES):
-                            for u in range(2):
-                                nc.tensor.transpose(w_t[:, m, u, :], words[:, m, g, u, :], ident_f32[:])
-                        grouped_words = w_grouped[:, g].bitcast(F32)
-                        if g == 0:
-                            nc.vector.tensor_copy(
-                                out=grouped_words, in_=w_t[:].rearrange("p m u d -> p m d u")
-                            )
-                        else:
-                            nc.scalar.copy(out=grouped_words, in_=w_t[:].rearrange("p m u d -> p m d u"))
-                    nc.vector.quantize_mx(
-                        out=w_codes[name][:].bitcast(FP8X4),
-                        scales=w_scales[name][:],
-                        in_=w_grouped[:].rearrange("p g m d j -> p (g m d j)"),
-                    )
-
-                frames = v_raw[:].rearrange("p j (t h w) -> p j t h w", h=H, w=W)
-                for half in range(2):
-                    row_sum = setup_psum.tile([P, 2, T, W], F32, tag="row_sum", bufs=2)
-                    for i in range(2):
-                        for h in range(H):
-                            nc.tensor.matmul(
-                                out=row_sum[:, i],
-                                lhsT=ident_bf16[:],
-                                rhs=frames[:, 2 * half + i, :, h, :],
-                                start=(h == 0),
-                                stop=(h == H - 1),
-                            )
-                    nc.vector.tensor_reduce(
-                        out=z_sum[:, 2 * half : 2 * half + 2, :], in_=row_sum[:], axis=AXIS_X, op=ADD
-                    )
-                z_cols = resident.tile([P, T, Z_COPIES, PACK], BF16, align_bytes=64)
-                nc.vector.tensor_scalar(
-                    out=z_cols[:],
-                    in0=z_sum[:].rearrange("p j t -> p t j").unsqueeze(2).to_broadcast([P, T, Z_COPIES, PACK]),
-                    scalar1=1.0 / (H * W),
-                    scalar2=None,
-                    op0=MULT,
-                )
-                nc.vector.memset(z_scales[:].bitcast(I32), 0)
+                for g in range(PASSES):
+                    w_t = psum.tile([P, D_TILES, 2, P], F32, tag="phi_psum")
+                    for m in range(D_TILES):
+                        for u in range(2):
+                            nc.tensor.transpose(w_t[:, m, u, :], words[:, m, g, u, :], ident_f32[:])
+                    grouped_words = w_grouped[name][:, g].bitcast(F32)
+                    if g == 0:
+                        nc.vector.tensor_copy(out=grouped_words, in_=w_t[:].rearrange("p m u d -> p m d u"))
+                    else:
+                        nc.scalar.copy(out=grouped_words, in_=w_t[:].rearrange("p m u d -> p m d u"))
+            for name in ("p", "g"):
                 nc.vector.quantize_mx(
-                    out=z_codes[:].bitcast(FP8X4),
-                    scales=z_scales[:],
-                    in_=z_cols[:].rearrange("p t c j -> p (t c j)"),
+                    out=w_codes[name][:].bitcast(FP8X4),
+                    scales=w_scales[name][:],
+                    in_=w_grouped[name][:].rearrange("p g m d j -> p (g m d j)"),
                 )
+            frames = v_raw[:].rearrange("p j (t h w) -> p j t h w", h=H, w=W)
 
-                bias_psum = setup_psum.tile([P, 2 * D], F32)
-                nc.tensor.matmul(
-                    out=bias_psum[:, 0:D], lhsT=ones[:], rhs=bias_rows[:, D : 2 * D], start=True, stop=True
-                )
-                for m in range(D_TILES):
+            def sum_frames(j):
+                row_sum = psum.tile([P, T, W], F32, tag="g_psum")
+                for h in range(H):
                     nc.tensor.matmul(
-                        out=bias_psum[:, D + 32 * m : D + 32 * (m + 1)],
-                        lhsT=bias_rows[:, m * P : (m + 1) * P],
-                        rhs=ones[:, 0:32],
-                        start=True,
-                        stop=True,
+                        out=row_sum[:],
+                        lhsT=ident_bf16[:],
+                        rhs=frames[:, j, :, h, :],
+                        start=(h == 0),
+                        stop=(h == H - 1),
                     )
-                nc.vector.tensor_copy(out=bg_all[:], in_=bias_psum[:, 0:D])
-                nc.vector.tensor_copy(
-                    out=bp_col[:],
-                    in_=bias_psum[:, D : D + 32 * D_TILES].rearrange("p (m n) -> p m n", n=32)[:, :, 0],
+                nc.vector.tensor_reduce(out=z_sum[:, j, :], in_=row_sum[:], axis=AXIS_X, op=ADD)
+
+            for j in range(PACK - 1):
+                sum_frames(j)
+            regroup(0)
+            sum_frames(PACK - 1)
+            quantise(0)
+
+            bias_psum = psum.tile([P, 2 * D], F32, tag="g_psum")
+            nc.tensor.matmul(
+                out=bias_psum[:, 0:D], lhsT=ones[:], rhs=bias_rows[:, D : 2 * D], start=True, stop=True
+            )
+            for m in range(D_TILES):
+                nc.tensor.matmul(
+                    out=bias_psum[:, D + 32 * m : D + 32 * (m + 1)],
+                    lhsT=bias_rows[:, m * P : (m + 1) * P],
+                    rhs=ones[:, 0:32],
+                    start=True,
+                    stop=True,
+                )
+            nc.scalar.copy(out=bg_all[:], in_=bias_psum[:, 0:D])
+            nc.scalar.copy(
+                out=bp_col[:],
+                in_=bias_psum[:, D : D + 32 * D_TILES].rearrange("p (m n) -> p m n", n=32)[:, :, 0],
+            )
+
+            nc.vector.tensor_scalar(
+                out=z_cols[:],
+                in0=z_sum[:].rearrange("p j t -> p t j").unsqueeze(2).to_broadcast([P, T, Z_COPIES, PACK]),
+                scalar1=1.0 / (H * W),
+                scalar2=None,
+                op0=MULT,
+            )
+            multiply_phi(0)
+            regroup(1)
+            nc.vector.quantize_mx(
+                out=z_codes[:].bitcast(FP8X4),
+                scales=z_scales[:],
+                in_=z_cols[:].rearrange("p t c j -> p (t c j)"),
+            )
+
+            z_phi = psum.tile([P, D_TILES, T, Z_COPIES], F32, tag="g_psum")
+            for m in range(D_TILES):
+                d_cols = slice(D + m * P, D + (m + 1) * P)
+                nc.tensor.matmul_mx(
+                    out=z_phi[:, m],
+                    lhsT=w_codes["p"][:, d_cols].bitcast(FP8X4),
+                    lhsT_scale=w_scales["p"][:, d_cols],
+                    rhs=z_codes[:].bitcast(FP8X4),
+                    rhs_scale=z_scales[:],
+                    start=True,
+                    stop=True,
                 )
 
+            def copy_z(first, steps):
+                columns = slice(first * P, (first + steps) * P)
+                z_columns = slice(first * Z_COPIES, (first + steps) * Z_COPIES)
                 nc.vector.tensor_copy(
-                    out=zz_codes[:].bitcast(I32).rearrange("p (t b c) -> p t b c", t=T, c=Z_COPIES),
-                    in_=z_codes[:]
+                    out=zz_codes[:, columns].bitcast(I32).rearrange("p (t b c) -> p t b c", t=steps, c=Z_COPIES),
+                    in_=z_codes[:, z_columns]
                     .bitcast(I32)
                     .rearrange("p (t c) -> p t c", c=Z_COPIES)
                     .unsqueeze(2)
-                    .to_broadcast([P, T, P // Z_COPIES, Z_COPIES]),
+                    .to_broadcast([P, steps, P // Z_COPIES, Z_COPIES]),
                 )
                 nc.vector.tensor_copy(
-                    out=zz_scales[:].bitcast(I32).rearrange("p (t b) -> p t b", t=T),
-                    in_=z_scales[:].bitcast(I32).unsqueeze(2).to_broadcast([P, T, P // Z_COPIES]),
+                    out=zz_scales[:, columns].bitcast(I32).rearrange("p (t b) -> p t b", t=steps),
+                    in_=z_scales[:, z_columns].bitcast(I32).unsqueeze(2).to_broadcast([P, steps, P // Z_COPIES]),
                 )
 
-                z_phi = setup_psum.tile([P, D_TILES, T, Z_COPIES], F32)
-                for m in range(D_TILES):
-                    d_cols = slice(D + m * P, D + (m + 1) * P)
-                    nc.tensor.matmul_mx(
-                        out=z_phi[:, m],
-                        lhsT=w_codes["p"][:, d_cols].bitcast(FP8X4),
-                        lhsT_scale=w_scales["p"][:, d_cols],
-                        rhs=z_codes[:].bitcast(FP8X4),
-                        rhs_scale=z_scales[:],
-                        start=True,
-                        stop=True,
-                    )
-                    nc.vector.tensor_scalar(
-                        out=phi_bias[:, m, :],
-                        in0=z_phi[:, m, :, 0],
-                        scalar1=bp_col[:, m : m + 1],
-                        scalar2=None,
-                        op0=ADD,
-                    )
+            copy_z(0, ZZ_PARTS[0])
+            nc.vector.tensor_tensor(
+                out=phi_bias[:],
+                in0=z_phi[:, :, :, 0],
+                in1=bp_col[:].unsqueeze(2).to_broadcast([P, D_TILES, T]),
+                op=ADD,
+            )
+            multiply_g(0)
 
-        with tc.tile_pool(name="g_pool", bufs=4) as g_pool, tc.psum_pool(
-            name="psum", bufs=4, reuse_waits="tile"
-        ) as psum:
-            grouped_of = {}
-            phi_psum_of = {}
-            g_psum_of = {}
-            phi_stage_of = {}
-            g_stage_of = {}
-            phi_chunk_of = {}
-            g_chunk_of = {}
-            for chunks, chunk_of in ((PHI_CHUNKS, phi_chunk_of), (G_CHUNKS, g_chunk_of)):
-                for steps in chunks:
-                    first = len(chunk_of)
-                    for t in range(first, first + steps):
-                        chunk_of[t] = (first, steps)
-
-            def regroup(t):
-                grouped = grouped_pool.tile([P, ROWS, P, PACK], BF16, tag="grouped", align_bytes=64)
-                dst = grouped[:].rearrange("p r m j -> p m j r")
-                src = a_step[t].rearrange("p j (m r) -> p m j r", r=ROWS)
-                nc.vector.tensor_copy(out=dst[:, 0:VECTOR_COLS], in_=src[:, 0:VECTOR_COLS])
-                nc.scalar.copy(out=dst[:, VECTOR_COLS:P], in_=src[:, VECTOR_COLS:P])
-                grouped_of[t] = grouped
-
-            def quantise_and_multiply(t):
-                a_codes = codes_pool.tile([P, STEP], U32, align_bytes=64)
-                a_scales = codes_pool.tile([P, STEP], U8, align_bytes=64)
-                nc.vector.quantize_mx(
-                    out=a_codes[:].bitcast(FP8X4),
-                    scales=a_scales[:],
-                    in_=grouped_of[t][:].rearrange("p r m j -> p (r m j)"),
-                )
-                phi_psum_of[t] = []
-                for m in range(D_TILES):
-                    phi_psum = psum.tile([P, STEP], F32)
-                    d_cols = slice(m * P, (m + 1) * P)
-                    nc.tensor.matmul_mx(
-                        out=phi_psum[:],
-                        lhsT=w_codes["p"][:, d_cols].bitcast(FP8X4),
-                        lhsT_scale=w_scales["p"][:, d_cols],
-                        rhs=a_codes[:].bitcast(FP8X4),
-                        rhs_scale=a_scales[:],
-                        start=True,
-                        stop=True,
-                    )
-                    phi_psum_of[t].append(phi_psum)
-                g_psum_of[t] = []
-                for pair in range(ROWS // 2):
-                    g_psum = psum.tile([P, 2, D], F32)
-                    for i in range(2):
-                        r = 2 * pair + i
-                        n_cols = slice(r * P, (r + 1) * P)
-                        z_cols_t = slice(t * P, (t + 1) * P)
-                        nc.tensor.matmul_mx(
-                            out=g_psum[:, i, :],
-                            lhsT=a_codes[:, n_cols].bitcast(FP8X4),
-                            lhsT_scale=a_scales[:, n_cols],
-                            rhs=w_codes["g"][:, 0:D].bitcast(FP8X4),
-                            rhs_scale=w_scales["g"][:, 0:D],
-                            start=True,
-                            stop=False,
-                        )
-                        nc.tensor.matmul_mx(
-                            out=g_psum[:, i, :],
-                            lhsT=zz_codes[:, z_cols_t].bitcast(FP8X4),
-                            lhsT_scale=zz_scales[:, z_cols_t],
-                            rhs=w_codes["g"][:, D : 2 * D].bitcast(FP8X4),
-                            rhs_scale=w_scales["g"][:, D : 2 * D],
-                            start=False,
-                            stop=True,
-                        )
-                    g_psum_of[t].append(g_psum)
+        with tc.tile_pool(name="g_pool", bufs=4) as g_pool:
 
             def finish(t):
                 first, steps = phi_chunk_of[t]
@@ -313,9 +323,7 @@ def tile_nlgate_pa_t_kernel(tc, v, a, Wp, bp, Wg, bg, out_0, out_1):
                     )
                 first, steps = g_chunk_of[t]
                 if t == first:
-                    g_stage = g_pool.tile(
-                        [P, steps, ROWS, D], F32, tag="g_stage", align_bytes=DMA_ALIGN
-                    )
+                    g_stage = g_pool.tile([P, steps, ROWS, D], F32, tag="g_stage", align_bytes=DMA_ALIGN)
                     g_stage_of[first] = g_stage
                 g_stage = g_stage_of[first]
                 for pair in range(ROWS // 2):
@@ -331,10 +339,13 @@ def tile_nlgate_pa_t_kernel(tc, v, a, Wp, bp, Wg, bg, out_0, out_1):
                         in_=g_stage[:].rearrange("p t r d -> p t (r d)"),
                     )
 
-            for t in range(-2, T):
+            for t in range(T):
                 if t + 2 < T:
                     regroup(t + 2)
-                if 0 <= t + 1 < T:
-                    quantise_and_multiply(t + 1)
-                if t >= 0:
-                    finish(t)
+                if t + 1 < T:
+                    quantise(t + 1)
+                    multiply_phi(t + 1)
+                    multiply_g(t + 1)
+                if t == 1:
+                    copy_z(ZZ_PARTS[0], ZZ_PARTS[1])
+                finish(t)

@@ -30,8 +30,8 @@ STEP = N // T
 D = 256
 D_TILES = D // P
 ROWS = STEP // P
-G_CHUNKS = (3, 3, 3, 3, 3, 1)
-PHI_CHUNKS = (2, 3, 3, 3, 3, 2)
+G_CHUNKS = (4, 4, 4, 4)
+PHI_CHUNKS = (2, 4, 4, 4, 2)
 A_PIECES = (2, 2, 4, 8)
 Z_COPIES = 4
 ZZ_PARTS = (4, 12)
@@ -46,12 +46,12 @@ def tile_nlgate_pa_t_kernel(tc, v, a, Wp, bp, Wg, bg, out_0, out_1):
 
     a_rows = a[0].rearrange("(p j) i f -> p j (i f)", j=PACK)
     v_rows = v[0].rearrange("(p j) t h w -> p j (t h w)", j=PACK)
-    phi_out = out_0[0].rearrange("(m p) n -> p m n", p=P)
+    phi_out = out_0[0].rearrange("(p m) n -> p m n", p=P)
     g_out = out_1[0].rearrange("(t c r) d -> c t (r d)", c=P, r=ROWS)
 
     with tc.tile_pool(name="resident", bufs=1) as resident, tc.tile_pool(
         name="grouped_pool", bufs=4
-    ) as grouped_pool, tc.tile_pool(name="phi_pool", bufs=4) as phi_pool, tc.tile_pool(
+    ) as grouped_pool, tc.tile_pool(name="phi_pool", bufs=3) as phi_pool, tc.tile_pool(
         name="codes_pool", bufs=4
     ) as codes_pool, tc.psum_pool(
         name="psum", bufs=4, reuse_waits="tile"
@@ -165,15 +165,15 @@ def tile_nlgate_pa_t_kernel(tc, v, a, Wp, bp, Wg, bg, out_0, out_1):
                 raw = load_pool.tile(
                     [P, D_TILES, PASSES * K_PASS], BF16, name="w_raw_%s" % name, align_bytes=DMA_ALIGN
                 )
-                nc.sync.dma_start(out=raw[:], in_=w.rearrange("(m p) k -> p m k", p=P))
+                nc.sync.dma_start(out=raw[:], in_=w.rearrange("(p m) k -> p m k", p=P))
                 w_raw[name] = raw
             v_raw = load_pool.tile([P, PACK, T * H * W], BF16, align_bytes=DMA_ALIGN)
             for half in range(2):
                 nc.sync.dma_start(
                     out=v_raw[:, 2 * half : 2 * half + 2, :], in_=v_rows[:, 2 * half : 2 * half + 2, :]
                 )
-            nc.sync.dma_start(out=bias_rows[0:1, 0:D], in_=bp.unsqueeze(0))
-            nc.sync.dma_start(out=bias_rows[0:1, D : 2 * D], in_=bg.unsqueeze(0))
+            nc.scalar.dma_start(out=bias_rows[0:1, 0:D], in_=bp.unsqueeze(0))
+            nc.scalar.dma_start(out=bias_rows[0:1, D : 2 * D], in_=bg.unsqueeze(0))
             a_step = []
             for piece_steps in A_PIECES:
                 first = len(a_step)
@@ -190,23 +190,29 @@ def tile_nlgate_pa_t_kernel(tc, v, a, Wp, bp, Wg, bg, out_0, out_1):
             for name in ("p", "g"):
                 words = w_raw[name][:].bitcast(F32).rearrange("p m (g q u) -> p m g u q", g=PASSES, u=2)
                 w_grouped[name] = grouped_pool.tile(
-                    [P, PASSES, D_TILES, P, PACK], BF16, name="w_grouped_%s" % name, tag="grouped", align_bytes=64
+                    [P, PASSES, D, PACK], BF16, name="w_grouped_%s" % name, tag="grouped", align_bytes=64
                 )
                 for g in range(PASSES):
                     w_t = psum.tile([P, D_TILES, 2, P], F32, tag="phi_psum")
                     for m in range(D_TILES):
                         for u in range(2):
                             nc.tensor.transpose(w_t[:, m, u, :], words[:, m, g, u, :], ident_f32[:])
-                    grouped_words = w_grouped[name][:, g].bitcast(F32)
-                    if g == 0:
-                        nc.vector.tensor_copy(out=grouped_words, in_=w_t[:].rearrange("p m u d -> p m d u"))
+                    target = w_grouped[name][:, g].bitcast(F32)
+                    if name == "p":
+                        target = target.rearrange("p (m q) u -> p m q u", m=D_TILES)
+                        source = w_t[:].rearrange("p m u q -> p m q u")
                     else:
-                        nc.scalar.copy(out=grouped_words, in_=w_t[:].rearrange("p m u d -> p m d u"))
+                        target = target.rearrange("p (q m) u -> p q m u", m=D_TILES)
+                        source = w_t[:].rearrange("p m u q -> p q m u")
+                    if g == 0:
+                        nc.vector.tensor_copy(out=target, in_=source)
+                    else:
+                        nc.scalar.copy(out=target, in_=source)
             for name in ("p", "g"):
                 nc.vector.quantize_mx(
                     out=w_codes[name][:].bitcast(FP8X4),
                     scales=w_scales[name][:],
-                    in_=w_grouped[name][:].rearrange("p g m d j -> p (g m d j)"),
+                    in_=w_grouped[name][:].rearrange("p g d j -> p (g d j)"),
                 )
             frames = v_raw[:].rearrange("p j (t h w) -> p j t h w", h=H, w=W)
 
@@ -235,7 +241,7 @@ def tile_nlgate_pa_t_kernel(tc, v, a, Wp, bp, Wg, bg, out_0, out_1):
             for m in range(D_TILES):
                 nc.tensor.matmul(
                     out=bias_psum[:, D + 32 * m : D + 32 * (m + 1)],
-                    lhsT=bias_rows[:, m * P : (m + 1) * P],
+                    lhsT=bias_rows[:, m:D:D_TILES],
                     rhs=ones[:, 0:32],
                     start=True,
                     stop=True,

@@ -30,6 +30,8 @@ STEP = N // T
 D = 256
 D_TILES = D // P
 ROWS = STEP // P
+PAIR = 2
+HALF_P = P // PAIR
 G_CHUNKS = (4, 4, 4, 4)
 PHI_CHUNKS = (2, 4, 4, 4, 2)
 A_PIECES = (2, 2, 4, 8)
@@ -47,7 +49,7 @@ def tile_nlgate_pa_t_kernel(tc, v, a, Wp, bp, Wg, bg, out_0, out_1):
     a_rows = a[0].rearrange("(p j) i f -> p j (i f)", j=PACK)
     v_rows = v[0].rearrange("(p j) t h w -> p j (t h w)", j=PACK)
     phi_out = out_0[0].rearrange("(p m) n -> p m n", p=P)
-    g_out = out_1[0].rearrange("(t c r) d -> c t (r d)", c=P, r=ROWS)
+    g_out = out_1[0].rearrange("(k c x) d -> c k (x d)", c=P, x=PAIR * ROWS)
 
     with tc.tile_pool(name="resident", bufs=1) as resident, tc.tile_pool(
         name="grouped_pool", bufs=4
@@ -75,8 +77,8 @@ def tile_nlgate_pa_t_kernel(tc, v, a, Wp, bp, Wg, bg, out_0, out_1):
         for name in ("p", "g"):
             w_codes[name] = resident.tile([P, PASSES * D], U32, name="w_codes_%s" % name, align_bytes=64)
             w_scales[name] = resident.tile([P, PASSES * D], U8, name="w_scales_%s" % name, align_bytes=64)
-        zz_codes = resident.tile([P, T * P], U32, align_bytes=64)
-        zz_scales = resident.tile([P, T * P], U8, align_bytes=64)
+        zz_codes = resident.tile([P, T * HALF_P], U32, align_bytes=64)
+        zz_scales = resident.tile([P, T * HALF_P], U8, align_bytes=64)
         z_codes = resident.tile([P, Z_COPIES * T], U32, align_bytes=64)
         z_scales = resident.tile([P, Z_COPIES * T], U8, align_bytes=64)
         z_cols = resident.tile([P, T, Z_COPIES, PACK], BF16, align_bytes=64)
@@ -88,27 +90,28 @@ def tile_nlgate_pa_t_kernel(tc, v, a, Wp, bp, Wg, bg, out_0, out_1):
         ident_bf16 = resident.tile([P, P], BF16)
         ident_f32 = resident.tile([P, P], F32)
 
-        def regroup(t):
+        def regroup(u):
+            k, b = divmod(u, PAIR)
             grouped = grouped_pool.tile([P, ROWS, P, PACK], BF16, tag="grouped", align_bytes=64)
             dst = grouped[:].rearrange("p r m j -> p m j r")
-            src = a_step[t].rearrange("p j (m r) -> p m j r", r=ROWS)
+            src = a_pair[k].rearrange("p j (m b r) -> p b m j r", b=PAIR, r=ROWS)[:, b]
             nc.vector.tensor_copy(out=dst[:, 0:VECTOR_COLS], in_=src[:, 0:VECTOR_COLS])
             nc.scalar.copy(out=dst[:, VECTOR_COLS:P], in_=src[:, VECTOR_COLS:P])
-            grouped_of[t] = grouped
+            grouped_of[u] = grouped
 
-        def quantise(t):
+        def quantise(u):
             a_codes = codes_pool.tile([P, STEP], U32, align_bytes=64)
             a_scales = codes_pool.tile([P, STEP], U8, align_bytes=64)
             nc.vector.quantize_mx(
                 out=a_codes[:].bitcast(FP8X4),
                 scales=a_scales[:],
-                in_=grouped_of[t][:].rearrange("p r m j -> p (r m j)"),
+                in_=grouped_of[u][:].rearrange("p r m j -> p (r m j)"),
             )
-            a_codes_of[t] = (a_codes, a_scales)
+            a_codes_of[u] = (a_codes, a_scales)
 
-        def multiply_phi(t):
-            a_codes, a_scales = a_codes_of[t]
-            phi_psum_of[t] = []
+        def multiply_phi(u):
+            a_codes, a_scales = a_codes_of[u]
+            phi_psum_of[u] = []
             for m in range(D_TILES):
                 phi_psum = psum.tile([P, STEP], F32, tag="phi_psum")
                 d_cols = slice(m * P, (m + 1) * P)
@@ -121,12 +124,13 @@ def tile_nlgate_pa_t_kernel(tc, v, a, Wp, bp, Wg, bg, out_0, out_1):
                     start=True,
                     stop=True,
                 )
-                phi_psum_of[t].append(phi_psum)
+                phi_psum_of[u].append(phi_psum)
 
-        def multiply_g(t):
-            a_codes, a_scales = a_codes_of[t]
-            z_cols_t = slice(t * P, (t + 1) * P)
-            g_psum_of[t] = []
+        def multiply_g(u):
+            a_codes, a_scales = a_codes_of[u]
+            k = u // PAIR
+            z_cols_k = slice(k * P, (k + 1) * P)
+            g_psum_of[u] = []
             for pair in range(ROWS // 2):
                 g_psum = psum.tile([P, 2, D], F32, tag="g_psum")
                 for i in range(2):
@@ -143,14 +147,14 @@ def tile_nlgate_pa_t_kernel(tc, v, a, Wp, bp, Wg, bg, out_0, out_1):
                     )
                     nc.tensor.matmul_mx(
                         out=g_psum[:, i, :],
-                        lhsT=zz_codes[:, z_cols_t].bitcast(FP8X4),
-                        lhsT_scale=zz_scales[:, z_cols_t],
+                        lhsT=zz_codes[:, z_cols_k].bitcast(FP8X4),
+                        lhsT_scale=zz_scales[:, z_cols_k],
                         rhs=w_codes["g"][:, D : 2 * D].bitcast(FP8X4),
                         rhs_scale=w_scales["g"][:, D : 2 * D],
                         start=False,
                         stop=True,
                     )
-                g_psum_of[t].append(g_psum)
+                g_psum_of[u].append(g_psum)
 
         with tc.tile_pool(name="load_pool", bufs=1) as load_pool:
             bias_rows = load_pool.tile([P, 2 * D], BF16)
@@ -174,17 +178,17 @@ def tile_nlgate_pa_t_kernel(tc, v, a, Wp, bp, Wg, bg, out_0, out_1):
                 )
             nc.scalar.dma_start(out=bias_rows[0:1, 0:D], in_=bp.unsqueeze(0))
             nc.scalar.dma_start(out=bias_rows[0:1, D : 2 * D], in_=bg.unsqueeze(0))
-            a_step = []
+            a_pair = []
             for piece_steps in A_PIECES:
-                first = len(a_step)
+                first = PAIR * len(a_pair)
                 raw = resident.tile(
                     [P, PACK, piece_steps * STEP], BF16, name="a_raw_%d" % first, align_bytes=DMA_ALIGN
                 )
                 nc.sync.dma_start(
                     out=raw[:], in_=a_rows[:, :, first * STEP : (first + piece_steps) * STEP]
                 )
-                for s in range(piece_steps):
-                    a_step.append(raw[:, :, s * STEP : (s + 1) * STEP])
+                for s in range(0, piece_steps, PAIR):
+                    a_pair.append(raw[:, :, s * STEP : (s + PAIR) * STEP])
 
             w_grouped = {}
             for name in ("p", "g"):
@@ -281,7 +285,7 @@ def tile_nlgate_pa_t_kernel(tc, v, a, Wp, bp, Wg, bg, out_0, out_1):
                 )
 
             def copy_z(first, steps):
-                columns = slice(first * P, (first + steps) * P)
+                columns = slice(first * HALF_P, (first + steps) * HALF_P)
                 z_columns = slice(first * Z_COPIES, (first + steps) * Z_COPIES)
                 nc.vector.tensor_copy(
                     out=zz_codes[:, columns].bitcast(I32).rearrange("p (t b c) -> p t b c", t=steps, c=Z_COPIES),
@@ -289,11 +293,11 @@ def tile_nlgate_pa_t_kernel(tc, v, a, Wp, bp, Wg, bg, out_0, out_1):
                     .bitcast(I32)
                     .rearrange("p (t c) -> p t c", c=Z_COPIES)
                     .unsqueeze(2)
-                    .to_broadcast([P, steps, P // Z_COPIES, Z_COPIES]),
+                    .to_broadcast([P, steps, HALF_P // Z_COPIES, Z_COPIES]),
                 )
                 nc.vector.tensor_copy(
                     out=zz_scales[:, columns].bitcast(I32).rearrange("p (t b) -> p t b", t=steps),
-                    in_=z_scales[:, z_columns].bitcast(I32).unsqueeze(2).to_broadcast([P, steps, P // Z_COPIES]),
+                    in_=z_scales[:, z_columns].bitcast(I32).unsqueeze(2).to_broadcast([P, steps, HALF_P // Z_COPIES]),
                 )
 
             copy_z(0, ZZ_PARTS[0])
@@ -307,51 +311,58 @@ def tile_nlgate_pa_t_kernel(tc, v, a, Wp, bp, Wg, bg, out_0, out_1):
 
         with tc.tile_pool(name="g_pool", bufs=4) as g_pool:
 
-            def finish(t):
-                first, steps = phi_chunk_of[t]
-                if t == first:
+            def finish(u):
+                k, b = divmod(u, PAIR)
+                first, steps = phi_chunk_of[PAIR * k]
+                if u == first:
                     phi_stage = phi_pool.tile(
                         [P, D_TILES, steps * STEP], F32, tag="phi_stage", align_bytes=DMA_ALIGN
                     )
                     phi_stage_of[first] = phi_stage
                 phi_stage = phi_stage_of[first]
-                stage_cols = slice((t - first) * STEP, (t - first + 1) * STEP)
                 for m in range(D_TILES):
-                    nc.scalar.activation(
-                        out=phi_stage[:, m, stage_cols].rearrange("p (c r) -> p c r", r=ROWS),
-                        in_=phi_psum_of[t][m][:].rearrange("p (r c) -> p c r", r=ROWS),
-                        func=IDENTITY,
-                        bias=phi_bias[:, m, t : t + 1],
-                    )
-                if t == first + steps - 1:
+                    banks = phi_psum_of[u][m][:].rearrange("p (r i c) -> p i c r", r=ROWS, i=PAIR)
+                    for i in range(PAIR):
+                        t = PAIR * k + i
+                        columns = phi_stage[:, m, (t - first) * STEP : (t - first + 1) * STEP]
+                        nc.scalar.activation(
+                            out=columns.rearrange("p (c b r) -> p b c r", b=PAIR, r=ROWS)[:, b],
+                            in_=banks[:, i],
+                            func=IDENTITY,
+                            bias=phi_bias[:, m, t : t + 1],
+                        )
+                if u == first + steps - 1:
                     nc.sync.dma_start(
                         out=phi_out[:, :, first * STEP : (first + steps) * STEP], in_=phi_stage[:]
                     )
-                first, steps = g_chunk_of[t]
-                if t == first:
-                    g_stage = g_pool.tile([P, steps, ROWS, D], F32, tag="g_stage", align_bytes=DMA_ALIGN)
+                first, steps = g_chunk_of[PAIR * k]
+                if u == first:
+                    g_stage = g_pool.tile(
+                        [P, steps // PAIR, PAIR * ROWS, D], F32, tag="g_stage", align_bytes=DMA_ALIGN
+                    )
                     g_stage_of[first] = g_stage
                 g_stage = g_stage_of[first]
-                for pair in range(ROWS // 2):
+                for q in range(ROWS // 2):
+                    x = ROWS * b + 2 * q
                     nc.vector.tensor_tensor(
-                        out=g_stage[:, t - first, 2 * pair : 2 * pair + 2, :],
-                        in0=g_psum_of[t][pair][:],
+                        out=g_stage[:, k - first // PAIR, x : x + 2, :],
+                        in0=g_psum_of[u][q][:],
                         in1=bg_all[:].unsqueeze(1).to_broadcast([P, 2, D]),
                         op=ADD,
                     )
-                if t == first + steps - 1:
+                if u == first + steps - 1:
                     nc.sync.dma_start(
-                        out=g_out[:, first : first + steps, :],
-                        in_=g_stage[:].rearrange("p t r d -> p t (r d)"),
+                        out=g_out[:, first // PAIR : (first + steps) // PAIR, :],
+                        in_=g_stage[:].rearrange("p k x d -> p k (x d)"),
                     )
 
-            for t in range(T):
-                if t + 2 < T:
-                    regroup(t + 2)
-                if t + 1 < T:
-                    quantise(t + 1)
-                    multiply_phi(t + 1)
-                    multiply_g(t + 1)
-                if t == 1:
+            for u in range(T):
+                if u + 2 < T:
+                    regroup(u + 2)
+                if u + 1 < T:
+                    quantise(u + 1)
+                    multiply_phi(u + 1)
+                    multiply_g(u + 1)
+                if u == 1:
                     copy_z(ZZ_PARTS[0], ZZ_PARTS[1])
-                finish(t)
+                finish(u)

@@ -176,8 +176,8 @@ def tile_nlgate_pa_t_kernel(tc, v, a, Wp, bp, Wg, bg, out_0, out_1):
                 nc.sync.dma_start(
                     out=v_raw[:, 2 * half : 2 * half + 2, :], in_=v_rows[:, 2 * half : 2 * half + 2, :]
                 )
-            nc.scalar.dma_start(out=bias_rows[0:1, 0:D], in_=bp.unsqueeze(0))
-            nc.scalar.dma_start(out=bias_rows[0:1, D : 2 * D], in_=bg.unsqueeze(0))
+            nc.sync.dma_start(out=bias_rows[0:1, 0:D], in_=bp.unsqueeze(0))
+            nc.sync.dma_start(out=bias_rows[0:1, D : 2 * D], in_=bg.unsqueeze(0))
             a_pair = []
             for piece_steps in A_PIECES:
                 first = PAIR * len(a_pair)
@@ -232,10 +232,16 @@ def tile_nlgate_pa_t_kernel(tc, v, a, Wp, bp, Wg, bg, out_0, out_1):
                     )
                 nc.vector.tensor_reduce(out=z_sum[:, j, :], in_=row_sum[:], axis=AXIS_X, op=ADD)
 
-            for j in range(PACK - 1):
-                sum_frames(j)
+            nc.vector.tensor_reduce(
+                out=z_sum[:, 1, :],
+                in_=v_raw[:, 1, :].rearrange("p (t x) -> p t x", t=T),
+                axis=AXIS_X,
+                op=ADD,
+            )
+            sum_frames(0)
+            sum_frames(2)
             regroup(0)
-            sum_frames(PACK - 1)
+            sum_frames(3)
             quantise(0)
 
             bias_psum = psum.tile([P, 2 * D], F32, tag="g_psum")

@@ -37,7 +37,7 @@ PHI_CHUNKS = (2, 4, 4, 4, 2)
 A_PIECES = (2, 2, 4, 8)
 Z_COPIES = 4
 ZZ_PARTS = (4, 12)
-DMA_ALIGN = 256
+DMA_ALIGN = 4096
 VECTOR_COLS = 64
 
 FLOPS = 2 * 2 * D * PASSES * K_PASS * N

import concourse.mybir as mybir
from concourse.masks import make_identity

BF16 = mybir.dt.bfloat16
F32 = mybir.dt.float32
U32 = mybir.dt.uint32
U8 = mybir.dt.uint8
I32 = mybir.dt.int32
FP8X4 = mybir.dt.float8_e4m3fn_x4
ADD = mybir.AluOpType.add
MULT = mybir.AluOpType.mult
IDENTITY = mybir.ActivationFunctionType.Identity
AXIS_X = mybir.AxisListType.X
ORDERED = {
    mybir.EngineType.SP,
    mybir.EngineType.PE,
    mybir.EngineType.DVE,
    mybir.EngineType.Activation,
}

P = 128
PACK = 4
K_PASS = P * PACK
PASSES = 2
T = 16
H = 14
W = 14
N = 8192
STEP = N // T
D = 256
D_TILES = D // P
ROWS = STEP // P
PAIR = 2
HALF_P = P // PAIR
G_CHUNKS = (4, 4, 4, 4)
PHI_CHUNKS = (2, 4, 4, 4, 2)
A_PIECES = (2, 2, 4, 8)
Z_COPIES = 4
ZZ_PARTS = (4, 12)
DMA_ALIGN = 4096
VECTOR_COLS = 64

FLOPS = 2 * 2 * D * PASSES * K_PASS * N


def tile_nlgate_pa_t_kernel(tc, v, a, Wp, bp, Wg, bg, out_0, out_1):
    nc = tc.nc

    a_rows = a[0].rearrange("(p j) i f -> p j (i f)", j=PACK)
    v_rows = v[0].rearrange("(p j) t h w -> p j (t h w)", j=PACK)
    phi_out = out_0[0].rearrange("(p m) n -> p m n", p=P)
    g_out = out_1[0].rearrange("(k c x) d -> c k (x d)", c=P, x=PAIR * ROWS)

    with tc.tile_pool(name="resident", bufs=1) as resident, tc.tile_pool(
        name="grouped_pool", bufs=4
    ) as grouped_pool, tc.tile_pool(name="phi_pool", bufs=3) as phi_pool, tc.tile_pool(
        name="codes_pool", bufs=4
    ) as codes_pool, tc.psum_pool(
        name="psum", bufs=4, reuse_waits="tile"
    ) as psum, tc.manual_schedule(engines=ORDERED):
        grouped_of = {}
        a_codes_of = {}
        phi_psum_of = {}
        g_psum_of = {}
        phi_stage_of = {}
        g_stage_of = {}
        phi_chunk_of = {}
        g_chunk_of = {}
        for chunks, chunk_of in ((PHI_CHUNKS, phi_chunk_of), (G_CHUNKS, g_chunk_of)):
            for steps in chunks:
                first = len(chunk_of)
                for t in range(first, first + steps):
                    chunk_of[t] = (first, steps)

        w_codes = {}
        w_scales = {}
        for name in ("p", "g"):
            w_codes[name] = resident.tile([P, PASSES * D], U32, name="w_codes_%s" % name, align_bytes=64)
            w_scales[name] = resident.tile([P, PASSES * D], U8, name="w_scales_%s" % name, align_bytes=64)
        zz_codes = resident.tile([P, T * HALF_P], U32, align_bytes=64)
        zz_scales = resident.tile([P, T * HALF_P], U8, align_bytes=64)
        z_codes = resident.tile([P, Z_COPIES * T], U32, align_bytes=64)
        z_scales = resident.tile([P, Z_COPIES * T], U8, align_bytes=64)
        z_cols = resident.tile([P, T, Z_COPIES, PACK], BF16, align_bytes=64)
        z_sum = resident.tile([P, PACK, T], F32)
        bg_all = resident.tile([P, D], F32)
        bp_col = resident.tile([P, D_TILES], F32)
        phi_bias = resident.tile([P, D_TILES, T], F32)
        ones = resident.tile([P, P], BF16)
        ident_bf16 = resident.tile([P, P], BF16)
        ident_f32 = resident.tile([P, P], F32)

        def regroup(u):
            k, b = divmod(u, PAIR)
            grouped = grouped_pool.tile([P, ROWS, P, PACK], BF16, tag="grouped", align_bytes=64)
            dst = grouped[:].rearrange("p r m j -> p m j r")
            src = a_pair[k].rearrange("p j (m b r) -> p b m j r", b=PAIR, r=ROWS)[:, b]
            nc.vector.tensor_copy(out=dst[:, 0:VECTOR_COLS], in_=src[:, 0:VECTOR_COLS])
            nc.scalar.copy(out=dst[:, VECTOR_COLS:P], in_=src[:, VECTOR_COLS:P])
            grouped_of[u] = grouped

        def quantise(u):
            a_codes = codes_pool.tile([P, STEP], U32, align_bytes=64)
            a_scales = codes_pool.tile([P, STEP], U8, align_bytes=64)
            nc.vector.quantize_mx(
                out=a_codes[:].bitcast(FP8X4),
                scales=a_scales[:],
                in_=grouped_of[u][:].rearrange("p r m j -> p (r m j)"),
            )
            a_codes_of[u] = (a_codes, a_scales)

        def multiply_phi(u):
            a_codes, a_scales = a_codes_of[u]
            phi_psum_of[u] = []
            for m in range(D_TILES):
                phi_psum = psum.tile([P, STEP], F32, tag="phi_psum")
                d_cols = slice(m * P, (m + 1) * P)
                nc.tensor.matmul_mx(
                    out=phi_psum[:],
                    lhsT=w_codes["p"][:, d_cols].bitcast(FP8X4),
                    lhsT_scale=w_scales["p"][:, d_cols],
                    rhs=a_codes[:].bitcast(FP8X4),
                    rhs_scale=a_scales[:],
                    start=True,
                    stop=True,
                )
                phi_psum_of[u].append(phi_psum)

        def multiply_g(u):
            a_codes, a_scales = a_codes_of[u]
            k = u // PAIR
            z_cols_k = slice(k * P, (k + 1) * P)
            g_psum_of[u] = []
            for pair in range(ROWS // 2):
                g_psum = psum.tile([P, 2, D], F32, tag="g_psum")
                for i in range(2):
                    r = 2 * pair + i
                    n_cols = slice(r * P, (r + 1) * P)
                    nc.tensor.matmul_mx(
                        out=g_psum[:, i, :],
                        lhsT=a_codes[:, n_cols].bitcast(FP8X4),
                        lhsT_scale=a_scales[:, n_cols],
                        rhs=w_codes["g"][:, 0:D].bitcast(FP8X4),
                        rhs_scale=w_scales["g"][:, 0:D],
                        start=True,
                        stop=False,
                    )
                    nc.tensor.matmul_mx(
                        out=g_psum[:, i, :],
                        lhsT=zz_codes[:, z_cols_k].bitcast(FP8X4),
                        lhsT_scale=zz_scales[:, z_cols_k],
                        rhs=w_codes["g"][:, D : 2 * D].bitcast(FP8X4),
                        rhs_scale=w_scales["g"][:, D : 2 * D],
                        start=False,
                        stop=True,
                    )
                g_psum_of[u].append(g_psum)

        with tc.tile_pool(name="load_pool", bufs=1) as load_pool:
            bias_rows = load_pool.tile([P, 2 * D], BF16)
            nc.vector.memset(bias_rows[:], 0.0)
            nc.vector.memset(ones[:], 1.0)
            nc.vector.memset(z_scales[:].bitcast(I32), 0)
            make_identity(nc, ident_f32[:])
            make_identity(nc, ident_bf16[:])

            w_raw = {}
            for name, w in (("p", Wp), ("g", Wg)):
                raw = load_pool.tile(
                    [P, D_TILES, PASSES * K_PASS], BF16, name="w_raw_%s" % name, align_bytes=DMA_ALIGN
                )
                nc.sync.dma_start(out=raw[:], in_=w.rearrange("(p m) k -> p m k", p=P))
                w_raw[name] = raw
            v_raw = load_pool.tile([P, PACK, T * H * W], BF16, align_bytes=DMA_ALIGN)
            for half in range(2):
                nc.sync.dma_start(
                    out=v_raw[:, 2 * half : 2 * half + 2, :], in_=v_rows[:, 2 * half : 2 * half + 2, :]
                )
            nc.sync.dma_start(out=bias_rows[0:1, 0:D], in_=bp.unsqueeze(0))
            nc.sync.dma_start(out=bias_rows[0:1, D : 2 * D], in_=bg.unsqueeze(0))
            a_pair = []
            for piece_steps in A_PIECES:
                first = PAIR * len(a_pair)
                raw = resident.tile(
                    [P, PACK, piece_steps * STEP], BF16, name="a_raw_%d" % first, align_bytes=DMA_ALIGN
                )
                nc.sync.dma_start(
                    out=raw[:], in_=a_rows[:, :, first * STEP : (first + piece_steps) * STEP]
                )
                for s in range(0, piece_steps, PAIR):
                    a_pair.append(raw[:, :, s * STEP : (s + PAIR) * STEP])

            w_grouped = {}
            for name in ("p", "g"):
                words = w_raw[name][:].bitcast(F32).rearrange("p m (g q u) -> p m g u q", g=PASSES, u=2)
                w_grouped[name] = grouped_pool.tile(
                    [P, PASSES, D, PACK], BF16, name="w_grouped_%s" % name, tag="grouped", align_bytes=64
                )
                for g in range(PASSES):
                    w_t = psum.tile([P, D_TILES, 2, P], F32, tag="phi_psum")
                    for m in range(D_TILES):
                        for u in range(2):
                            nc.tensor.transpose(w_t[:, m, u, :], words[:, m, g, u, :], ident_f32[:])
                    target = w_grouped[name][:, g].bitcast(F32)
                    if name == "p":
                        target = target.rearrange("p (m q) u -> p m q u", m=D_TILES)
                        source = w_t[:].rearrange("p m u q -> p m q u")
                    else:
                        target = target.rearrange("p (q m) u -> p q m u", m=D_TILES)
                        source = w_t[:].rearrange("p m u q -> p q m u")
                    if g == 0:
                        nc.vector.tensor_copy(out=target, in_=source)
                    else:
                        nc.scalar.copy(out=target, in_=source)
            for name in ("p", "g"):
                nc.vector.quantize_mx(
                    out=w_codes[name][:].bitcast(FP8X4),
                    scales=w_scales[name][:],
                    in_=w_grouped[name][:].rearrange("p g d j -> p (g d j)"),
                )
            frames = v_raw[:].rearrange("p j (t h w) -> p j t h w", h=H, w=W)

            def sum_frames(j):
                row_sum = psum.tile([P, T, W], F32, tag="g_psum")
                for h in range(H):
                    nc.tensor.matmul(
                        out=row_sum[:],
                        lhsT=ident_bf16[:],
                        rhs=frames[:, j, :, h, :],
                        start=(h == 0),
                        stop=(h == H - 1),
                    )
                nc.vector.tensor_reduce(out=z_sum[:, j, :], in_=row_sum[:], axis=AXIS_X, op=ADD)

            nc.vector.tensor_reduce(
                out=z_sum[:, 1, :],
                in_=v_raw[:, 1, :].rearrange("p (t x) -> p t x", t=T),
                axis=AXIS_X,
                op=ADD,
            )
            sum_frames(0)
            sum_frames(2)
            regroup(0)
            sum_frames(3)
            quantise(0)

            bias_psum = psum.tile([P, 2 * D], F32, tag="g_psum")
            nc.tensor.matmul(
                out=bias_psum[:, 0:D], lhsT=ones[:], rhs=bias_rows[:, D : 2 * D], start=True, stop=True
            )
            for m in range(D_TILES):
                nc.tensor.matmul(
                    out=bias_psum[:, D + 32 * m : D + 32 * (m + 1)],
                    lhsT=bias_rows[:, m:D:D_TILES],
                    rhs=ones[:, 0:32],
                    start=True,
                    stop=True,
                )
            nc.scalar.copy(out=bg_all[:], in_=bias_psum[:, 0:D])
            nc.scalar.copy(
                out=bp_col[:],
                in_=bias_psum[:, D : D + 32 * D_TILES].rearrange("p (m n) -> p m n", n=32)[:, :, 0],
            )

            nc.vector.tensor_scalar(
                out=z_cols[:],
                in0=z_sum[:].rearrange("p j t -> p t j").unsqueeze(2).to_broadcast([P, T, Z_COPIES, PACK]),
                scalar1=1.0 / (H * W),
                scalar2=None,
                op0=MULT,
            )
            multiply_phi(0)
            regroup(1)
            nc.vector.quantize_mx(
                out=z_codes[:].bitcast(FP8X4),
                scales=z_scales[:],
                in_=z_cols[:].rearrange("p t c j -> p (t c j)"),
            )

            z_phi = psum.tile([P, D_TILES, T, Z_COPIES], F32, tag="g_psum")
            for m in range(D_TILES):
                d_cols = slice(D + m * P, D + (m + 1) * P)
                nc.tensor.matmul_mx(
                    out=z_phi[:, m],
                    lhsT=w_codes["p"][:, d_cols].bitcast(FP8X4),
                    lhsT_scale=w_scales["p"][:, d_cols],
                    rhs=z_codes[:].bitcast(FP8X4),
                    rhs_scale=z_scales[:],
                    start=True,
                    stop=True,
                )

            def copy_z(first, steps):
                columns = slice(first * HALF_P, (first + steps) * HALF_P)
                z_columns = slice(first * Z_COPIES, (first + steps) * Z_COPIES)
                nc.vector.tensor_copy(
                    out=zz_codes[:, columns].bitcast(I32).rearrange("p (t b c) -> p t b c", t=steps, c=Z_COPIES),
                    in_=z_codes[:, z_columns]
                    .bitcast(I32)
                    .rearrange("p (t c) -> p t c", c=Z_COPIES)
                    .unsqueeze(2)
                    .to_broadcast([P, steps, HALF_P // Z_COPIES, Z_COPIES]),
                )
                nc.vector.tensor_copy(
                    out=zz_scales[:, columns].bitcast(I32).rearrange("p (t b) -> p t b", t=steps),
                    in_=z_scales[:, z_columns].bitcast(I32).unsqueeze(2).to_broadcast([P, steps, HALF_P // Z_COPIES]),
                )

            copy_z(0, ZZ_PARTS[0])
            nc.vector.tensor_tensor(
                out=phi_bias[:],
                in0=z_phi[:, :, :, 0],
                in1=bp_col[:].unsqueeze(2).to_broadcast([P, D_TILES, T]),
                op=ADD,
            )
            multiply_g(0)

        with tc.tile_pool(name="g_pool", bufs=4) as g_pool:

            def finish(u):
                k, b = divmod(u, PAIR)
                first, steps = phi_chunk_of[PAIR * k]
                if u == first:
                    phi_stage = phi_pool.tile(
                        [P, D_TILES, steps * STEP], F32, tag="phi_stage", align_bytes=DMA_ALIGN
                    )
                    phi_stage_of[first] = phi_stage
                phi_stage = phi_stage_of[first]
                for m in range(D_TILES):
                    banks = phi_psum_of[u][m][:].rearrange("p (r i c) -> p i c r", r=ROWS, i=PAIR)
                    for i in range(PAIR):
                        t = PAIR * k + i
                        columns = phi_stage[:, m, (t - first) * STEP : (t - first + 1) * STEP]
                        nc.scalar.activation(
                            out=columns.rearrange("p (c b r) -> p b c r", b=PAIR, r=ROWS)[:, b],
                            in_=banks[:, i],
                            func=IDENTITY,
                            bias=phi_bias[:, m, t : t + 1],
                        )
                if u == first + steps - 1:
                    nc.sync.dma_start(
                        out=phi_out[:, :, first * STEP : (first + steps) * STEP], in_=phi_stage[:]
                    )
                first, steps = g_chunk_of[PAIR * k]
                if u == first:
                    g_stage = g_pool.tile(
                        [P, steps // PAIR, PAIR * ROWS, D], F32, tag="g_stage", align_bytes=DMA_ALIGN
                    )
                    g_stage_of[first] = g_stage
                g_stage = g_stage_of[first]
                for q in range(ROWS // 2):
                    x = ROWS * b + 2 * q
                    nc.vector.tensor_tensor(
                        out=g_stage[:, k - first // PAIR, x : x + 2, :],
                        in0=g_psum_of[u][q][:],
                        in1=bg_all[:].unsqueeze(1).to_broadcast([P, 2, D]),
                        op=ADD,
                    )
                if u == first + steps - 1:
                    nc.sync.dma_start(
                        out=g_out[:, first // PAIR : (first + steps) // PAIR, :],
                        in_=g_stage[:].rearrange("p k x d -> p k (x d)"),
                    )

            for u in range(T):
                if u + 2 < T:
                    regroup(u + 2)
                if u + 1 < T:
                    quantise(u + 1)
                    multiply_phi(u + 1)
                    multiply_g(u + 1)
                if u == 1:
                    copy_z(ZZ_PARTS[0], ZZ_PARTS[1])
                finish(u)
